import numpy as np
import ml_dtypes


def mxq(x, axis, fmt="e4m3"):
    dtype, down = {"e4m3": (ml_dtypes.float8_e4m3fn, 7), "e5m2": (ml_dtypes.float8_e5m2, 14)}[fmt]
    v = np.moveaxis(np.asarray(x, np.float32).astype(ml_dtypes.bfloat16).astype(np.float64), axis, -1)
    blocks = v.reshape(v.shape[:-1] + (-1, 32))
    amax = np.abs(blocks).max(-1, keepdims=True)
    byte = np.maximum(np.where(amax > 0, np.frexp(amax)[1] - 1 + 127, 0) - down, 1)
    scale = np.exp2(byte - 127.0)
    codes = (blocks / scale).astype(np.float32).astype(dtype).astype(np.float64)
    return np.moveaxis((codes * scale).reshape(v.shape), -1, axis)


WIDE = False


def mx_kscale(k):
    if not WIDE:
        return np.ones(k)
    levels = np.array([10, -10, 5, -5, 0])
    a = np.random.permutation(np.resize(levels, k // 512 * 4)).reshape(k // 512, 4)
    idx = np.arange(k)
    return np.exp2(a[idx // 512, idx % 128 // 32])


BF16 = ml_dtypes.bfloat16


def bf(x):
    return np.asarray(x, np.float32).astype(BF16)


def f64(x):
    return np.asarray(x).astype(np.float64)


E2M1 = np.array([0.0, 0.5, 1.0, 1.5, 2.0, 3.0, 4.0, 6.0, -0.0, -0.5, -1.0, -1.5, -2.0, -3.0, -4.0, -6.0])


def pack_weight(w, fmt):
    k, n = w.shape
    w = f64(bf(w)).reshape(k // 32, 32, n)
    amax = np.abs(w).max(1)
    if fmt == "e4m3":
        byte = np.frexp(amax)[1] - 1 + 127 - 7
    else:
        mant, ex = np.frexp(amax / 6.0)
        byte = np.where(mant > 0.5, ex, ex - 1) + 127
    byte = np.clip(np.where(amax > 0, byte, 1), 1, 254)
    scaled = (w * np.exp2(127.0 - byte)[:, None, :]).reshape(k, n).astype(np.float32)
    by_word = np.ascontiguousarray(scaled.reshape(k // 512, 128, 4, n).transpose(0, 1, 3, 2))
    if fmt == "e4m3":
        words = by_word.astype(ml_dtypes.float8_e4m3fn).view(np.uint8)
    else:
        c = by_word.astype(ml_dtypes.float4_e2m1fn).view(np.uint8) & 0xF
        words = c[..., 0::2] | (c[..., 1::2] << 4)
    return np.ascontiguousarray(words), np.ascontiguousarray(byte.astype(np.uint8).reshape(k // 512, 16, n))


def unpack_weight(words, scales, fmt):
    g, p, n, _ = words.shape
    if fmt == "e4m3":
        vals = np.ascontiguousarray(words).view(ml_dtypes.float8_e4m3fn).astype(np.float64)
    else:
        nib = np.empty((g, p, n, 4), np.uint8)
        nib[..., 0::2] = words & 0xF
        nib[..., 1::2] = words >> 4
        vals = E2M1[nib]
    vals = vals * np.repeat(np.exp2(scales.astype(np.float64) - 127.0), 8, axis=1)[..., None]
    return vals.transpose(0, 1, 3, 2).reshape(g * 512, n)

def pack4(w):
    words, scales = pack_weight(w, "e2m1")
    return words.reshape(words.shape[0], 128, -1), scales


def unpack4(words, scales):
    return unpack_weight(words.reshape(words.shape[0], 128, -1, 2), scales, "e2m1")


B, D, F, A, M = 8192, 1024, 512, 32, 256
G = 11.0


def setup_inputs():
    s = mx_kscale(D)
    r = 0.5 + np.random.random_sample((B, 1))
    next_state = bf(np.random.standard_normal((B, D)) * r * s)
    seen = bf(np.maximum(np.random.standard_normal((M, F)), 0.0) * G / np.sqrt(F))
    wf = np.random.standard_normal((F, D)) * G / np.sqrt(D * F) / s
    words, scales = pack4(np.ascontiguousarray(wf.T))
    b_feat = bf(np.random.standard_normal(F) * 0.5 * G / np.sqrt(F))
    return {"next_state": next_state,
            "seen": seen,
            "Wf_words": words,
            "Wf_scales": scales,
            "b_feat": b_feat}


def reference(next_state, seen, Wf_words, Wf_scales, b_feat):
    mem = f64(seen)
    fa = np.maximum((mxq(f64(next_state), 1, "e4m3") @ unpack4(Wf_words, Wf_scales)) + f64(b_feat), 0.0)
    a2 = np.sum(fa ** 2, axis=-1, keepdims=True)
    s2 = np.sum(mem ** 2, axis=-1)
    d2 = a2 + s2[None, :] - 2.0 * (mxq(fa, 1, "e4m3") @ mxq(mem, 1, "e4m3").T)
    min_dist = np.sqrt(np.maximum(np.min(d2, axis=-1), 0.0))
    return np.minimum(1.0, min_dist / 10.0)

@@ -1,0 +1,245 @@
+from contextlib import ExitStack
+
+import concourse.mybir as mybir
+from concourse.masks import make_identity
+
+F32 = mybir.dt.float32
+BF16 = mybir.dt.bfloat16
+I32 = mybir.dt.int32
+U32 = mybir.dt.uint32
+U8 = mybir.dt.uint8
+FP8X4 = mybir.dt.float8_e4m3fn_x4
+FP4X4 = mybir.dt.float4_e2m1fn_x4
+ACT = mybir.ActivationFunctionType
+ALU = mybir.AluOpType
+
+P = 128
+PACK = 4
+STATES, STATE_DIM, FEATURES, MEMORY = 8192, 1024, 512, 256
+K_PASSES = STATE_DIM // (P * PACK)
+GROUPS = STATES // P
+PAIRS = GROUPS // 2
+PAIR_STATES = 2 * P
+BLOCK_STATES = 4 * P
+MEMORY_HALVES = MEMORY // P
+X_BLOCKS_AHEAD = 3
+TRANSPOSE_LEAD = 3
+QUANTISE_LEAD = 2
+REGROUP_LAG = 2
+DISTANCE_LAG = 3
+SQRT_FLOOR = 1e-30
+
+FLOPS = 2 * STATES * STATE_DIM * FEATURES + 2 * STATES * FEATURES * MEMORY
+
+
+def tile_curiositymodule_pa_t_kernel(tc, next_state, seen, Wf_words, Wf_scales, b_feat, out):
+    nc = tc.nc
+    x_rows = next_state.rearrange("(p c) k -> p c k", c=GROUPS)
+
+    with ExitStack() as ctx:
+        ctx.enter_context(tc.manual_schedule())
+        keep = ctx.enter_context(tc.tile_pool(name="keep", bufs=1))
+        x_pool = ctx.enter_context(tc.tile_pool(name="x", bufs=X_BLOCKS_AHEAD + 1))
+        ring3 = ctx.enter_context(tc.tile_pool(name="ring3", bufs=3))
+        ring2 = ctx.enter_context(tc.tile_pool(name="ring2", bufs=2))
+
+        x_blocks, x_grouped, x_codes, x_scales = {}, {}, {}, {}
+        fa_blocks, fa_codes, fa_scales = {}, {}, {}
+
+        def load_block(block):
+            x_sb = x_pool.tile([P, 4, STATE_DIM], BF16)
+            nc.sync.dma_start(out=x_sb[:], in_=x_rows[:, 4 * block : 4 * block + 4, :])
+            x_blocks[block] = x_sb
+
+        load_block(0)
+
+        ident_f32 = keep.tile([P, P], F32)
+        make_identity(nc, ident_f32[:])
+        ident_bf16 = keep.tile([P, P], BF16)
+        make_identity(nc, ident_bf16[:])
+
+        w_words = keep.tile([P, K_PASSES, 2 * FEATURES], U8, align_bytes=64)
+        nc.sync.dma_start(out=w_words[:].bitcast(I32), in_=Wf_words.bitcast(I32).rearrange("g p b -> p g b"))
+        w_scales = keep.tile([P, K_PASSES, FEATURES], U8, align_bytes=64)
+        nc.vector.memset(w_scales[:].bitcast(I32), 0)
+        for quadrant in range(4):
+            nc.sync.dma_start(
+                out=w_scales[32 * quadrant : 32 * quadrant + 4].bitcast(I32),
+                in_=Wf_scales[:, 4 * quadrant : 4 * quadrant + 4, :].bitcast(I32).rearrange("g r n -> r g n"),
+            )
+        for block in range(1, X_BLOCKS_AHEAD):
+            load_block(block)
+
+        seen_sb = keep.tile([P, MEMORY_HALVES, FEATURES], BF16)
+        nc.scalar.dma_start(out=seen_sb[:], in_=seen.rearrange("(c m) j -> m c j", m=P))
+        bias_rows = keep.tile([P, P], BF16)
+        nc.vector.memset(bias_rows[:], 0.0)
+        nc.scalar.dma_start(out=bias_rows[0:PACK, :], in_=b_feat.rearrange("(t p) -> t p", p=P))
+
+        one = keep.tile([P, 1], F32)
+        nc.vector.memset(one[:], 1.0)
+        nc.scalar.activation(out=one[:], in_=one[:], func=ACT.Sqrt)
+
+        bias = keep.tile([P, PACK], F32)
+        half_s2 = keep.tile([P, MEMORY], F32)
+        seen_grouped = keep.tile([P, MEMORY, PACK], BF16, align_bytes=64)
+        seen_codes = keep.tile([P, MEMORY], U32, align_bytes=64)
+        seen_scales = keep.tile([P, MEMORY], U8, align_bytes=64)
+        s2 = keep.tile([P, MEMORY_HALVES], F32)
+        with tc.psum_pool(name="setup_psum", bufs=1) as setup_psum:
+            bias_ps = setup_psum.tile([P, P], BF16)
+            nc.tensor.transpose(bias_ps[:], bias_rows[:], ident_bf16[:])
+            nc.vector.tensor_copy(out=bias[:], in_=bias_ps[:, 0:PACK])
+
+            for c in range(MEMORY_HALVES):
+                seen_ps = setup_psum.tile([P, PACK, P], BF16, bufs=2)
+                for t in range(PACK):
+                    nc.tensor.transpose(seen_ps[:, t, :], seen_sb[:, c, t * P : (t + 1) * P], ident_bf16[:])
+                nc.vector.tensor_copy(
+                    out=seen_grouped[:, c * P : (c + 1) * P, :], in_=seen_ps[:].rearrange("p t m -> p m t")
+                )
+
+            s2_ps = setup_psum.tile([P, MEMORY_HALVES, P], F32)
+            for c in range(MEMORY_HALVES):
+                seen_squares = ring2.tile([P, FEATURES], F32)
+                nc.scalar.activation(
+                    out=seen_squares[:], in_=seen_sb[:, c, :], func=ACT.Square, accum_out=s2[:, c : c + 1]
+                )
+                s2_repeated = ring2.tile([P, P], F32)
+                nc.vector.tensor_copy(out=s2_repeated[:], in_=s2[:, c : c + 1].to_broadcast([P, P]))
+                nc.tensor.transpose(s2_ps[:, c, :], s2_repeated[:], ident_f32[:])
+            nc.vector.tensor_scalar_mul(out=half_s2[:], in0=s2_ps[:].rearrange("p c m -> p (c m)"), scalar1=0.5)
+            nc.vector.quantize_mx(
+                out=seen_codes[:].bitcast(FP8X4),
+                scales=seen_scales[:],
+                in_=seen_grouped[:].rearrange("p m t -> p (m t)"),
+            )
+
+        a2 = keep.tile([P, GROUPS], F32)
+        best = keep.tile([P, GROUPS], F32)
+
+        xt_psum = ctx.enter_context(tc.psum_pool(name="xt_psum", bufs=2))
+        ft_psum = ctx.enter_context(tc.psum_pool(name="ft_psum", bufs=2))
+        z_psum = ctx.enter_context(tc.psum_pool(name="z_psum", bufs=2))
+        dot_psum = ctx.enter_context(tc.psum_pool(name="dot_psum", bufs=2))
+
+        def transpose_states(pair):
+            grouped = ring3.tile([P, K_PASSES, PAIR_STATES, 2], F32, name="x_grouped", align_bytes=64)
+            x_grouped[pair] = grouped
+            for i in range(2):
+                words = x_blocks[pair // 2][:, 2 * (pair % 2) + i, :].bitcast(F32)
+                xt = xt_psum.tile([P, K_PASSES, 2, P], F32)
+                for g in range(K_PASSES):
+                    for u in range(2):
+                        nc.tensor.transpose(xt[:, g, u, :], words[:, 256 * g + u : 256 * (g + 1) : 2], ident_f32[:])
+                copy = nc.vector.tensor_copy if i == 0 else nc.scalar.copy
+                copy(out=grouped[:, :, i * P : (i + 1) * P, :], in_=xt[:].rearrange("p g u s -> p g s u"))
+
+        def quantise_states(pair):
+            block, half = pair // 2, pair % 2
+            if half == 0:
+                codes = ring3.tile([P, K_PASSES, BLOCK_STATES], U32, name="x_codes", align_bytes=64)
+                scales = ring3.tile([P, K_PASSES, BLOCK_STATES], U8, name="x_scales", align_bytes=64)
+                x_codes[block], x_scales[block] = codes, scales
+            cols = slice(half * PAIR_STATES, (half + 1) * PAIR_STATES)
+            for g in range(K_PASSES):
+                nc.vector.quantize_mx(
+                    out=x_codes[block][:, g, cols].bitcast(FP8X4),
+                    scales=x_scales[block][:, g, cols],
+                    in_=x_grouped[pair][:, g].rearrange("p s u -> p (s u)").bitcast(BF16),
+                )
+
+        def features(block, t):
+            if t == 0:
+                fa = ring3.tile([P, PACK, BLOCK_STATES], F32, name="fa")
+                fa_blocks[block] = fa
+            z = z_psum.tile([P, BLOCK_STATES], F32)
+            for g in range(K_PASSES):
+                nc.tensor.matmul_mx(
+                    out=z[:],
+                    lhsT=w_words[:, g, 2 * P * t : 2 * P * (t + 1)].bitcast(FP4X4),
+                    lhsT_scale=w_scales[:, g, P * t : P * (t + 1)],
+                    rhs=x_codes[block][:, g, :].bitcast(FP8X4),
+                    rhs_scale=x_scales[block][:, g, :],
+                    start=(g == 0),
+                    stop=(g == K_PASSES - 1),
+                )
+            nc.scalar.activation(out=fa_blocks[block][:, t, :], in_=z[:], func=ACT.Relu, bias=bias[:, t : t + 1])
+
+        def regroup_features(pair):
+            cols = slice((pair % 2) * PAIR_STATES, (pair % 2 + 1) * PAIR_STATES)
+            grouped = ring2.tile([P, PAIR_STATES, PACK], BF16, name="fa_grouped", align_bytes=64)
+            nc.vector.tensor_copy(out=grouped[:], in_=fa_blocks[pair // 2][:, :, cols].rearrange("p t s -> p s t"))
+            return grouped
+
+        def quantise_features(pair, grouped):
+            codes = ring3.tile([P, PAIR_STATES], U32, name="fa_codes", align_bytes=64)
+            scales = ring3.tile([P, PAIR_STATES], U8, name="fa_scales", align_bytes=64)
+            nc.vector.quantize_mx(
+                out=codes[:].bitcast(FP8X4), scales=scales[:], in_=grouped[:].rearrange("p s t -> p (s t)")
+            )
+            fa_codes[pair], fa_scales[pair] = codes, scales
+
+        def square_norms(pair):
+            for i in range(2):
+                cols = slice((2 * (pair % 2) + i) * P, (2 * (pair % 2) + i + 1) * P)
+                ft = ft_psum.tile([P, PACK, P], F32)
+                for t in range(PACK):
+                    nc.tensor.transpose(ft[:, t, :], fa_blocks[pair // 2][:, t, cols], ident_f32[:])
+                squares = ring2.tile([P, FEATURES], F32)
+                nc.scalar.activation(
+                    out=squares[:],
+                    in_=ft[:].rearrange("p t f -> p (t f)"),
+                    func=ACT.Square,
+                    accum_out=a2[:, 2 * pair + i : 2 * pair + i + 1],
+                )
+
+        def distances(pair):
+            dot = dot_psum.tile([P, 2, MEMORY], F32)
+            for i in range(2):
+                nc.tensor.matmul_mx(
+                    out=dot[:, i, :],
+                    lhsT=fa_codes[pair][:, i * P : (i + 1) * P].bitcast(FP8X4),
+                    lhsT_scale=fa_scales[pair][:, i * P : (i + 1) * P],
+                    rhs=seen_codes[:].bitcast(FP8X4),
+                    rhs_scale=seen_scales[:],
+                    start=True,
+                    stop=True,
+                )
+            margin = ring2.tile([P, 2, MEMORY], F32)
+            nc.vector.tensor_tensor(
+                out=margin[:], in0=dot[:], in1=half_s2[:].unsqueeze(1).to_broadcast([P, 2, MEMORY]), op=ALU.subtract
+            )
+            nc.vector.tensor_reduce(
+                out=best[:, 2 * pair : 2 * pair + 2], in_=margin[:], axis=mybir.AxisListType.X, op=ALU.max
+            )
+
+        def is_pair(pair):
+            return 0 <= pair < PAIRS
+
+        for step in range(-TRANSPOSE_LEAD, PAIRS + DISTANCE_LAG):
+            ahead = step + TRANSPOSE_LEAD
+            if is_pair(ahead):
+                if ahead % 2 == 0 and ahead // 2 + X_BLOCKS_AHEAD < PAIRS // 2:
+                    load_block(ahead // 2 + X_BLOCKS_AHEAD)
+                transpose_states(ahead)
+            if is_pair(step - DISTANCE_LAG):
+                square_norms(step - DISTANCE_LAG)
+            fa_grouped = regroup_features(step - REGROUP_LAG) if is_pair(step - REGROUP_LAG) else None
+            if is_pair(step + QUANTISE_LEAD):
+                quantise_states(step + QUANTISE_LEAD)
+            if is_pair(step - REGROUP_LAG):
+                quantise_features(step - REGROUP_LAG, fa_grouped)
+            if is_pair(step):
+                features(step // 2, 2 * (step % 2))
+                features(step // 2, 2 * (step % 2) + 1)
+            if is_pair(step - DISTANCE_LAG):
+                distances(step - DISTANCE_LAG)
+
+        d2 = keep.tile([P, GROUPS], F32)
+        nc.vector.scalar_tensor_tensor(out=d2[:], in0=best[:], scalar=-2.0, in1=a2[:], op0=ALU.mult, op1=ALU.add)
+        nc.vector.tensor_scalar_max(out=d2[:], in0=d2[:], scalar1=SQRT_FLOOR)
+        novelty = keep.tile([P, GROUPS], F32)
+        nc.scalar.activation(out=novelty[:], in_=d2[:], func=ACT.Sqrt)
+        nc.vector.tensor_scalar(out=novelty[:], in0=novelty[:], scalar1=0.1, scalar2=1.0, op0=ALU.mult, op1=ALU.min)
+        nc.sync.dma_start(out=out.rearrange("(p c) -> p c", c=GROUPS), in_=novelty[:])

@@ -22,11 +22,14 @@ PAIRS = GROUPS // 2
 PAIR_STATES = 2 * P
 BLOCK_STATES = 4 * P
 MEMORY_HALVES = MEMORY // P
-X_BLOCKS_AHEAD = 3
+X_BUFS = 6
 TRANSPOSE_LEAD = 3
 QUANTISE_LEAD = 2
 REGROUP_LAG = 2
-DISTANCE_LAG = 3
+NORM_LAG = 3
+QUANTISE_LAG = 3
+DISTANCE_LAG = 4
+BEST_LAG = 5
 SQRT_FLOOR = 1e-30
 
 FLOPS = 2 * STATES * STATE_DIM * FEATURES + 2 * STATES * FEATURES * MEMORY
@@ -39,24 +42,25 @@ def tile_curiositymodule_pa_t_kernel(tc, next_state, seen, Wf_words, Wf_scales, 
     with ExitStack() as ctx:
         ctx.enter_context(tc.manual_schedule())
         keep = ctx.enter_context(tc.tile_pool(name="keep", bufs=1))
-        x_pool = ctx.enter_context(tc.tile_pool(name="x", bufs=X_BLOCKS_AHEAD + 1))
+        x_pool = ctx.enter_context(tc.tile_pool(name="x", bufs=X_BUFS))
         ring3 = ctx.enter_context(tc.tile_pool(name="ring3", bufs=3))
         ring2 = ctx.enter_context(tc.tile_pool(name="ring2", bufs=2))
+        psum = ctx.enter_context(tc.psum_pool(name="psum", bufs=2))
 
-        x_blocks, x_grouped, x_codes, x_scales = {}, {}, {}, {}
-        fa_blocks, fa_codes, fa_scales = {}, {}, {}
+        x_pairs, x_grouped, x_codes, x_scales = {}, {}, {}, {}
+        fa_blocks, fa_grouped, fa_codes, fa_scales, margins = {}, {}, {}, {}, {}
 
-        def load_block(block):
-            x_sb = x_pool.tile([P, 4, STATE_DIM], BF16)
-            nc.sync.dma_start(out=x_sb[:], in_=x_rows[:, 4 * block : 4 * block + 4, :])
-            x_blocks[block] = x_sb
+        def load_pair(pair):
+            x_sb = x_pool.tile([P, 2, STATE_DIM], BF16)
+            nc.sync.dma_start(out=x_sb[:], in_=x_rows[:, 2 * pair : 2 * pair + 2, :])
+            x_pairs[pair] = x_sb
 
-        load_block(0)
+        load_pair(0)
 
-        ident_f32 = keep.tile([P, P], F32)
-        make_identity(nc, ident_f32[:])
         ident_bf16 = keep.tile([P, P], BF16)
         make_identity(nc, ident_bf16[:])
+        ident_f32 = keep.tile([P, P], F32)
+        make_identity(nc, ident_f32[:])
 
         w_words = keep.tile([P, K_PASSES, 2 * FEATURES], U8, align_bytes=64)
         nc.sync.dma_start(out=w_words[:].bitcast(I32), in_=Wf_words.bitcast(I32).rearrange("g p b -> p g b"))
@@ -67,8 +71,8 @@ def tile_curiositymodule_pa_t_kernel(tc, next_state, seen, Wf_words, Wf_scales, 
                 out=w_scales[32 * quadrant : 32 * quadrant + 4].bitcast(I32),
                 in_=Wf_scales[:, 4 * quadrant : 4 * quadrant + 4, :].bitcast(I32).rearrange("g r n -> r g n"),
             )
-        for block in range(1, X_BLOCKS_AHEAD):
-            load_block(block)
+        for pair in range(1, X_BUFS - 1):
+            load_pair(pair)
 
         seen_sb = keep.tile([P, MEMORY_HALVES, FEATURES], BF16)
         nc.scalar.dma_start(out=seen_sb[:], in_=seen.rearrange("(c m) j -> m c j", m=P))
@@ -81,54 +85,49 @@ def tile_curiositymodule_pa_t_kernel(tc, next_state, seen, Wf_words, Wf_scales, 
         nc.scalar.activation(out=one[:], in_=one[:], func=ACT.Sqrt)
 
         bias = keep.tile([P, PACK], F32)
-        half_s2 = keep.tile([P, MEMORY], F32)
+        bias_ps = psum.tile([P, P], BF16, tag="dot")
+        nc.tensor.transpose(bias_ps[:], bias_rows[:], ident_bf16[:])
+        nc.vector.tensor_copy(out=bias[:], in_=bias_ps[:, 0:PACK])
+
         seen_grouped = keep.tile([P, MEMORY, PACK], BF16, align_bytes=64)
         seen_codes = keep.tile([P, MEMORY], U32, align_bytes=64)
         seen_scales = keep.tile([P, MEMORY], U8, align_bytes=64)
+        for c in range(MEMORY_HALVES):
+            seen_ps = psum.tile([P, PACK, P], BF16, tag="ft")
+            for t in range(PACK):
+                nc.tensor.transpose(seen_ps[:, t, :], seen_sb[:, c, t * P : (t + 1) * P], ident_bf16[:])
+            nc.vector.tensor_copy(
+                out=seen_grouped[:, c * P : (c + 1) * P, :], in_=seen_ps[:].rearrange("p t m -> p m t")
+            )
+        nc.vector.quantize_mx(
+            out=seen_codes[:].bitcast(FP8X4), scales=seen_scales[:], in_=seen_grouped[:].rearrange("p m t -> p (m t)")
+        )
+
         s2 = keep.tile([P, MEMORY_HALVES], F32)
-        with tc.psum_pool(name="setup_psum", bufs=1) as setup_psum:
-            bias_ps = setup_psum.tile([P, P], BF16)
-            nc.tensor.transpose(bias_ps[:], bias_rows[:], ident_bf16[:])
-            nc.vector.tensor_copy(out=bias[:], in_=bias_ps[:, 0:PACK])
+        for c in range(MEMORY_HALVES):
+            seen_squares = ring2.tile([P, FEATURES], F32)
+            nc.scalar.activation(
+                out=seen_squares[:], in_=seen_sb[:, c, :], func=ACT.Square, accum_out=s2[:, c : c + 1]
+            )
+        half_s2 = keep.tile([P, MEMORY], F32)
 
+        def spread_memory_norms():
+            s2_ps = psum.tile([P, MEMORY_HALVES, P], F32, tag="dot")
             for c in range(MEMORY_HALVES):
-                seen_ps = setup_psum.tile([P, PACK, P], BF16, bufs=2)
-                for t in range(PACK):
-                    nc.tensor.transpose(seen_ps[:, t, :], seen_sb[:, c, t * P : (t + 1) * P], ident_bf16[:])
-                nc.vector.tensor_copy(
-                    out=seen_grouped[:, c * P : (c + 1) * P, :], in_=seen_ps[:].rearrange("p t m -> p m t")
-                )
-
-            s2_ps = setup_psum.tile([P, MEMORY_HALVES, P], F32)
-            for c in range(MEMORY_HALVES):
-                seen_squares = ring2.tile([P, FEATURES], F32)
-                nc.scalar.activation(
-                    out=seen_squares[:], in_=seen_sb[:, c, :], func=ACT.Square, accum_out=s2[:, c : c + 1]
-                )
                 s2_repeated = ring2.tile([P, P], F32)
                 nc.vector.tensor_copy(out=s2_repeated[:], in_=s2[:, c : c + 1].to_broadcast([P, P]))
                 nc.tensor.transpose(s2_ps[:, c, :], s2_repeated[:], ident_f32[:])
             nc.vector.tensor_scalar_mul(out=half_s2[:], in0=s2_ps[:].rearrange("p c m -> p (c m)"), scalar1=0.5)
-            nc.vector.quantize_mx(
-                out=seen_codes[:].bitcast(FP8X4),
-                scales=seen_scales[:],
-                in_=seen_grouped[:].rearrange("p m t -> p (m t)"),
-            )
 
         a2 = keep.tile([P, GROUPS], F32)
         best = keep.tile([P, GROUPS], F32)
-
-        xt_psum = ctx.enter_context(tc.psum_pool(name="xt_psum", bufs=2))
-        ft_psum = ctx.enter_context(tc.psum_pool(name="ft_psum", bufs=2))
-        z_psum = ctx.enter_context(tc.psum_pool(name="z_psum", bufs=2))
-        dot_psum = ctx.enter_context(tc.psum_pool(name="dot_psum", bufs=2))
 
         def transpose_states(pair):
             grouped = ring3.tile([P, K_PASSES, PAIR_STATES, 2], F32, name="x_grouped", align_bytes=64)
             x_grouped[pair] = grouped
             for i in range(2):
-                words = x_blocks[pair // 2][:, 2 * (pair % 2) + i, :].bitcast(F32)
-                xt = xt_psum.tile([P, K_PASSES, 2, P], F32)
+                words = x_pairs[pair][:, i, :].bitcast(F32)
+                xt = psum.tile([P, K_PASSES, 2, P], F32)
                 for g in range(K_PASSES):
                     for u in range(2):
                         nc.tensor.transpose(xt[:, g, u, :], words[:, 256 * g + u : 256 * (g + 1) : 2], ident_f32[:])
@@ -151,9 +150,9 @@ def tile_curiositymodule_pa_t_kernel(tc, next_state, seen, Wf_words, Wf_scales, 
 
         def features(block, t):
             if t == 0:
-                fa = ring3.tile([P, PACK, BLOCK_STATES], F32, name="fa")
+                fa = ring3.tile([P, PACK, BLOCK_STATES], F32)
                 fa_blocks[block] = fa
-            z = z_psum.tile([P, BLOCK_STATES], F32)
+            z = psum.tile([P, BLOCK_STATES], F32)
             for g in range(K_PASSES):
                 nc.tensor.matmul_mx(
                     out=z[:],
@@ -168,22 +167,29 @@ def tile_curiositymodule_pa_t_kernel(tc, next_state, seen, Wf_words, Wf_scales, 
 
         def regroup_features(pair):
             cols = slice((pair % 2) * PAIR_STATES, (pair % 2 + 1) * PAIR_STATES)
-            grouped = ring2.tile([P, PAIR_STATES, PACK], BF16, name="fa_grouped", align_bytes=64)
-            nc.vector.tensor_copy(out=grouped[:], in_=fa_blocks[pair // 2][:, :, cols].rearrange("p t s -> p s t"))
-            return grouped
+            grouped = keep.tile([P, PAIR_STATES, PACK], BF16, name="fa_grouped", align_bytes=64)
+            nc.gpsimd.tensor_scalar(
+                out=grouped[:],
+                in0=fa_blocks[pair // 2][:, :, cols].rearrange("p t s -> p s t"),
+                scalar1=1.0,
+                scalar2=0.0,
+                op0=ALU.mult,
+                op1=ALU.add,
+            )
+            fa_grouped[pair] = grouped
 
-        def quantise_features(pair, grouped):
+        def quantise_features(pair):
             codes = ring3.tile([P, PAIR_STATES], U32, name="fa_codes", align_bytes=64)
             scales = ring3.tile([P, PAIR_STATES], U8, name="fa_scales", align_bytes=64)
             nc.vector.quantize_mx(
-                out=codes[:].bitcast(FP8X4), scales=scales[:], in_=grouped[:].rearrange("p s t -> p (s t)")
+                out=codes[:].bitcast(FP8X4), scales=scales[:], in_=fa_grouped[pair][:].rearrange("p s t -> p (s t)")
             )
             fa_codes[pair], fa_scales[pair] = codes, scales
 
         def square_norms(pair):
             for i in range(2):
                 cols = slice((2 * (pair % 2) + i) * P, (2 * (pair % 2) + i + 1) * P)
-                ft = ft_psum.tile([P, PACK, P], F32)
+                ft = psum.tile([P, PACK, P], F32)
                 for t in range(PACK):
                     nc.tensor.transpose(ft[:, t, :], fa_blocks[pair // 2][:, t, cols], ident_f32[:])
                 squares = ring2.tile([P, FEATURES], F32)
@@ -195,7 +201,7 @@ def tile_curiositymodule_pa_t_kernel(tc, next_state, seen, Wf_words, Wf_scales, 
                 )
 
         def distances(pair):
-            dot = dot_psum.tile([P, 2, MEMORY], F32)
+            dot = psum.tile([P, 2, MEMORY], F32)
             for i in range(2):
                 nc.tensor.matmul_mx(
                     out=dot[:, i, :],
@@ -210,31 +216,42 @@ def tile_curiositymodule_pa_t_kernel(tc, next_state, seen, Wf_words, Wf_scales, 
             nc.vector.tensor_tensor(
                 out=margin[:], in0=dot[:], in1=half_s2[:].unsqueeze(1).to_broadcast([P, 2, MEMORY]), op=ALU.subtract
             )
+            margins[pair] = margin
+
+        def nearest(pair):
             nc.vector.tensor_reduce(
-                out=best[:, 2 * pair : 2 * pair + 2], in_=margin[:], axis=mybir.AxisListType.X, op=ALU.max
+                out=best[:, 2 * pair : 2 * pair + 2], in_=margins[pair][:], axis=mybir.AxisListType.X, op=ALU.max
             )
 
         def is_pair(pair):
             return 0 <= pair < PAIRS
 
-        for step in range(-TRANSPOSE_LEAD, PAIRS + DISTANCE_LAG):
-            ahead = step + TRANSPOSE_LEAD
-            if is_pair(ahead):
-                if ahead % 2 == 0 and ahead // 2 + X_BLOCKS_AHEAD < PAIRS // 2:
-                    load_block(ahead // 2 + X_BLOCKS_AHEAD)
-                transpose_states(ahead)
-            if is_pair(step - DISTANCE_LAG):
-                square_norms(step - DISTANCE_LAG)
-            fa_grouped = regroup_features(step - REGROUP_LAG) if is_pair(step - REGROUP_LAG) else None
+        def pipeline_step(step):
+            if is_pair(step + TRANSPOSE_LEAD + X_BUFS - 1):
+                load_pair(step + TRANSPOSE_LEAD + X_BUFS - 1)
+            if is_pair(step + TRANSPOSE_LEAD):
+                transpose_states(step + TRANSPOSE_LEAD)
+            if is_pair(step - NORM_LAG):
+                square_norms(step - NORM_LAG)
+            if is_pair(step - BEST_LAG):
+                nearest(step - BEST_LAG)
             if is_pair(step + QUANTISE_LEAD):
                 quantise_states(step + QUANTISE_LEAD)
+            if is_pair(step - QUANTISE_LAG):
+                quantise_features(step - QUANTISE_LAG)
             if is_pair(step - REGROUP_LAG):
-                quantise_features(step - REGROUP_LAG, fa_grouped)
+                regroup_features(step - REGROUP_LAG)
             if is_pair(step):
                 features(step // 2, 2 * (step % 2))
                 features(step // 2, 2 * (step % 2) + 1)
             if is_pair(step - DISTANCE_LAG):
                 distances(step - DISTANCE_LAG)
+
+        for step in range(-TRANSPOSE_LEAD, 0):
+            pipeline_step(step)
+        spread_memory_norms()
+        for step in range(0, PAIRS + BEST_LAG):
+            pipeline_step(step)
 
         d2 = keep.tile([P, GROUPS], F32)
         nc.vector.scalar_tensor_tensor(out=d2[:], in0=best[:], scalar=-2.0, in1=a2[:], op0=ALU.mult, op1=ALU.add)

@@ -23,13 +23,15 @@ PAIR_STATES = 2 * P
 BLOCK_STATES = 4 * P
 MEMORY_HALVES = MEMORY // P
 X_BUFS = 6
+SORT_LEAD = 4
 TRANSPOSE_LEAD = 3
 QUANTISE_LEAD = 2
 REGROUP_LAG = 2
-NORM_LAG = 3
+NORM_LAG = 5
 QUANTISE_LAG = 3
 DISTANCE_LAG = 4
 BEST_LAG = 5
+LOAD_LEAD = TRANSPOSE_LEAD + X_BUFS - 1
 SQRT_FLOOR = 1e-30
 
 FLOPS = 2 * STATES * STATE_DIM * FEATURES + 2 * STATES * FEATURES * MEMORY
@@ -43,11 +45,12 @@ def tile_curiositymodule_pa_t_kernel(tc, next_state, seen, Wf_words, Wf_scales, 
         ctx.enter_context(tc.manual_schedule())
         keep = ctx.enter_context(tc.tile_pool(name="keep", bufs=1))
         x_pool = ctx.enter_context(tc.tile_pool(name="x", bufs=X_BUFS))
+        fa_pool = ctx.enter_context(tc.tile_pool(name="fa", bufs=4))
         ring3 = ctx.enter_context(tc.tile_pool(name="ring3", bufs=3))
         ring2 = ctx.enter_context(tc.tile_pool(name="ring2", bufs=2))
         psum = ctx.enter_context(tc.psum_pool(name="psum", bufs=2))
 
-        x_pairs, x_grouped, x_codes, x_scales = {}, {}, {}, {}
+        x_pairs, x_sorted, x_grouped, x_codes, x_scales = {}, {}, {}, {}, {}
         fa_blocks, fa_grouped, fa_codes, fa_scales, margins = {}, {}, {}, {}, {}
 
         def load_pair(pair):
@@ -71,7 +74,7 @@ def tile_curiositymodule_pa_t_kernel(tc, next_state, seen, Wf_words, Wf_scales, 
                 out=w_scales[32 * quadrant : 32 * quadrant + 4].bitcast(I32),
                 in_=Wf_scales[:, 4 * quadrant : 4 * quadrant + 4, :].bitcast(I32).rearrange("g r n -> r g n"),
             )
-        for pair in range(1, X_BUFS - 1):
+        for pair in range(1, LOAD_LEAD - SORT_LEAD):
             load_pair(pair)
 
         seen_sb = keep.tile([P, MEMORY_HALVES, FEATURES], BF16)
@@ -122,6 +125,14 @@ def tile_curiositymodule_pa_t_kernel(tc, next_state, seen, Wf_words, Wf_scales, 
         a2 = keep.tile([P, GROUPS], F32)
         best = keep.tile([P, GROUPS], F32)
 
+        def sort_words(pair):
+            ordered = ring2.tile([P, K_PASSES, 2, P], F32, name="x_sorted")
+            nc.vector.tensor_copy(
+                out=ordered[:],
+                in_=x_pairs[pair][:, 0, :].bitcast(F32).rearrange("p (g q u) -> p g u q", g=K_PASSES, u=2),
+            )
+            x_sorted[pair] = ordered
+
         def transpose_states(pair):
             grouped = ring3.tile([P, K_PASSES, PAIR_STATES, 2], F32, name="x_grouped", align_bytes=64)
             x_grouped[pair] = grouped
@@ -130,7 +141,11 @@ def tile_curiositymodule_pa_t_kernel(tc, next_state, seen, Wf_words, Wf_scales, 
                 xt = psum.tile([P, K_PASSES, 2, P], F32)
                 for g in range(K_PASSES):
                     for u in range(2):
-                        nc.tensor.transpose(xt[:, g, u, :], words[:, 256 * g + u : 256 * (g + 1) : 2], ident_f32[:])
+                        if i == 0:
+                            every_second = x_sorted[pair][:, g, u, :]
+                        else:
+                            every_second = words[:, 256 * g + u : 256 * (g + 1) : 2]
+                        nc.tensor.transpose(xt[:, g, u, :], every_second, ident_f32[:])
                 copy = nc.vector.tensor_copy if i == 0 else nc.scalar.copy
                 copy(out=grouped[:, :, i * P : (i + 1) * P, :], in_=xt[:].rearrange("p g u s -> p g s u"))
 
@@ -150,7 +165,7 @@ def tile_curiositymodule_pa_t_kernel(tc, next_state, seen, Wf_words, Wf_scales, 
 
         def features(block, t):
             if t == 0:
-                fa = ring3.tile([P, PACK, BLOCK_STATES], F32)
+                fa = fa_pool.tile([P, PACK, BLOCK_STATES], F32)
                 fa_blocks[block] = fa
             z = psum.tile([P, BLOCK_STATES], F32)
             for g in range(K_PASSES):
@@ -227,14 +242,16 @@ def tile_curiositymodule_pa_t_kernel(tc, next_state, seen, Wf_words, Wf_scales, 
             return 0 <= pair < PAIRS
 
         def pipeline_step(step):
-            if is_pair(step + TRANSPOSE_LEAD + X_BUFS - 1):
-                load_pair(step + TRANSPOSE_LEAD + X_BUFS - 1)
+            if is_pair(step + LOAD_LEAD):
+                load_pair(step + LOAD_LEAD)
             if is_pair(step + TRANSPOSE_LEAD):
                 transpose_states(step + TRANSPOSE_LEAD)
             if is_pair(step - NORM_LAG):
                 square_norms(step - NORM_LAG)
             if is_pair(step - BEST_LAG):
                 nearest(step - BEST_LAG)
+            if is_pair(step + SORT_LEAD):
+                sort_words(step + SORT_LEAD)
             if is_pair(step + QUANTISE_LEAD):
                 quantise_states(step + QUANTISE_LEAD)
             if is_pair(step - QUANTISE_LAG):
@@ -247,10 +264,10 @@ def tile_curiositymodule_pa_t_kernel(tc, next_state, seen, Wf_words, Wf_scales, 
             if is_pair(step - DISTANCE_LAG):
                 distances(step - DISTANCE_LAG)
 
-        for step in range(-TRANSPOSE_LEAD, 0):
+        for step in range(-SORT_LEAD, 0):
             pipeline_step(step)
         spread_memory_norms()
-        for step in range(0, PAIRS + BEST_LAG):
+        for step in range(0, PAIRS + max(BEST_LAG, NORM_LAG)):
             pipeline_step(step)
 
         d2 = keep.tile([P, GROUPS], F32)

@@ -23,7 +23,6 @@ PAIR_STATES = 2 * P
 BLOCK_STATES = 4 * P
 MEMORY_HALVES = MEMORY // P
 X_BUFS = 6
-SORT_LEAD = 4
 TRANSPOSE_LEAD = 3
 QUANTISE_LEAD = 2
 REGROUP_LAG = 2
@@ -31,7 +30,6 @@ NORM_LAG = 5
 QUANTISE_LAG = 3
 DISTANCE_LAG = 4
 BEST_LAG = 5
-LOAD_LEAD = TRANSPOSE_LEAD + X_BUFS - 1
 SQRT_FLOOR = 1e-30
 
 FLOPS = 2 * STATES * STATE_DIM * FEATURES + 2 * STATES * FEATURES * MEMORY
@@ -50,7 +48,7 @@ def tile_curiositymodule_pa_t_kernel(tc, next_state, seen, Wf_words, Wf_scales, 
         ring2 = ctx.enter_context(tc.tile_pool(name="ring2", bufs=2))
         psum = ctx.enter_context(tc.psum_pool(name="psum", bufs=2))
 
-        x_pairs, x_sorted, x_grouped, x_codes, x_scales = {}, {}, {}, {}, {}
+        x_pairs, x_grouped, x_codes, x_scales = {}, {}, {}, {}
         fa_blocks, fa_grouped, fa_codes, fa_scales, margins = {}, {}, {}, {}, {}
 
         def load_pair(pair):
@@ -74,23 +72,18 @@ def tile_curiositymodule_pa_t_kernel(tc, next_state, seen, Wf_words, Wf_scales, 
                 out=w_scales[32 * quadrant : 32 * quadrant + 4].bitcast(I32),
                 in_=Wf_scales[:, 4 * quadrant : 4 * quadrant + 4, :].bitcast(I32).rearrange("g r n -> r g n"),
             )
-        for pair in range(1, LOAD_LEAD - SORT_LEAD):
+        for pair in range(1, X_BUFS - 1):
             load_pair(pair)
 
-        seen_sb = keep.tile([P, MEMORY_HALVES, FEATURES], BF16)
-        nc.scalar.dma_start(out=seen_sb[:], in_=seen.rearrange("(c m) j -> m c j", m=P))
         bias_rows = keep.tile([P, P], BF16)
         nc.vector.memset(bias_rows[:], 0.0)
         nc.scalar.dma_start(out=bias_rows[0:PACK, :], in_=b_feat.rearrange("(t p) -> t p", p=P))
+        seen_sb = keep.tile([P, MEMORY_HALVES, FEATURES], BF16)
+        nc.scalar.dma_start(out=seen_sb[:], in_=seen.rearrange("(c m) j -> m c j", m=P))
 
         one = keep.tile([P, 1], F32)
         nc.vector.memset(one[:], 1.0)
         nc.scalar.activation(out=one[:], in_=one[:], func=ACT.Sqrt)
-
-        bias = keep.tile([P, PACK], F32)
-        bias_ps = psum.tile([P, P], BF16, tag="dot")
-        nc.tensor.transpose(bias_ps[:], bias_rows[:], ident_bf16[:])
-        nc.vector.tensor_copy(out=bias[:], in_=bias_ps[:, 0:PACK])
 
         seen_grouped = keep.tile([P, MEMORY, PACK], BF16, align_bytes=64)
         seen_codes = keep.tile([P, MEMORY], U32, align_bytes=64)
@@ -113,8 +106,12 @@ def tile_curiositymodule_pa_t_kernel(tc, next_state, seen, Wf_words, Wf_scales, 
                 out=seen_squares[:], in_=seen_sb[:, c, :], func=ACT.Square, accum_out=s2[:, c : c + 1]
             )
         half_s2 = keep.tile([P, MEMORY], F32)
+        bias = keep.tile([P, PACK], F32)
 
-        def spread_memory_norms():
+        def turn_small_vectors():
+            bias_ps = psum.tile([P, P], BF16, tag="dot")
+            nc.tensor.transpose(bias_ps[:], bias_rows[:], ident_bf16[:])
+            nc.vector.tensor_copy(out=bias[:], in_=bias_ps[:, 0:PACK])
             s2_ps = psum.tile([P, MEMORY_HALVES, P], F32, tag="dot")
             for c in range(MEMORY_HALVES):
                 s2_repeated = ring2.tile([P, P], F32)
@@ -125,14 +122,6 @@ def tile_curiositymodule_pa_t_kernel(tc, next_state, seen, Wf_words, Wf_scales, 
         a2 = keep.tile([P, GROUPS], F32)
         best = keep.tile([P, GROUPS], F32)
 
-        def sort_words(pair):
-            ordered = ring2.tile([P, K_PASSES, 2, P], F32, name="x_sorted")
-            nc.vector.tensor_copy(
-                out=ordered[:],
-                in_=x_pairs[pair][:, 0, :].bitcast(F32).rearrange("p (g q u) -> p g u q", g=K_PASSES, u=2),
-            )
-            x_sorted[pair] = ordered
-
         def transpose_states(pair):
             grouped = ring3.tile([P, K_PASSES, PAIR_STATES, 2], F32, name="x_grouped", align_bytes=64)
             x_grouped[pair] = grouped
@@ -141,11 +130,7 @@ def tile_curiositymodule_pa_t_kernel(tc, next_state, seen, Wf_words, Wf_scales, 
                 xt = psum.tile([P, K_PASSES, 2, P], F32)
                 for g in range(K_PASSES):
                     for u in range(2):
-                        if i == 0:
-                            every_second = x_sorted[pair][:, g, u, :]
-                        else:
-                            every_second = words[:, 256 * g + u : 256 * (g + 1) : 2]
-                        nc.tensor.transpose(xt[:, g, u, :], every_second, ident_f32[:])
+                        nc.tensor.transpose(xt[:, g, u, :], words[:, 256 * g + u : 256 * (g + 1) : 2], ident_f32[:])
                 copy = nc.vector.tensor_copy if i == 0 else nc.scalar.copy
                 copy(out=grouped[:, :, i * P : (i + 1) * P, :], in_=xt[:].rearrange("p g u s -> p g s u"))
 
@@ -242,16 +227,14 @@ def tile_curiositymodule_pa_t_kernel(tc, next_state, seen, Wf_words, Wf_scales, 
             return 0 <= pair < PAIRS
 
         def pipeline_step(step):
-            if is_pair(step + LOAD_LEAD):
-                load_pair(step + LOAD_LEAD)
+            if is_pair(step + TRANSPOSE_LEAD + X_BUFS - 1):
+                load_pair(step + TRANSPOSE_LEAD + X_BUFS - 1)
             if is_pair(step + TRANSPOSE_LEAD):
                 transpose_states(step + TRANSPOSE_LEAD)
             if is_pair(step - NORM_LAG):
                 square_norms(step - NORM_LAG)
             if is_pair(step - BEST_LAG):
                 nearest(step - BEST_LAG)
-            if is_pair(step + SORT_LEAD):
-                sort_words(step + SORT_LEAD)
             if is_pair(step + QUANTISE_LEAD):
                 quantise_states(step + QUANTISE_LEAD)
             if is_pair(step - QUANTISE_LAG):
@@ -264,9 +247,9 @@ def tile_curiositymodule_pa_t_kernel(tc, next_state, seen, Wf_words, Wf_scales, 
             if is_pair(step - DISTANCE_LAG):
                 distances(step - DISTANCE_LAG)
 
-        for step in range(-SORT_LEAD, 0):
+        for step in range(-TRANSPOSE_LEAD, 0):
             pipeline_step(step)
-        spread_memory_norms()
+        turn_small_vectors()
         for step in range(0, PAIRS + max(BEST_LAG, NORM_LAG)):
             pipeline_step(step)
 

@@ -22,14 +22,9 @@ PAIRS = GROUPS // 2
 PAIR_STATES = 2 * P
 BLOCK_STATES = 4 * P
 MEMORY_HALVES = MEMORY // P
-X_BUFS = 6
-TRANSPOSE_LEAD = 3
-QUANTISE_LEAD = 2
-REGROUP_LAG = 2
-NORM_LAG = 5
-QUANTISE_LAG = 3
-DISTANCE_LAG = 4
-BEST_LAG = 5
+BLOCK_GROUPS = 4
+BLOCKS = GROUPS // BLOCK_GROUPS
+X_BUFS = 8
 SQRT_FLOOR = 1e-30
 
 FLOPS = 2 * STATES * STATE_DIM * FEATURES + 2 * STATES * FEATURES * MEMORY
@@ -43,28 +38,32 @@ def tile_curiositymodule_pa_t_kernel(tc, next_state, seen, Wf_words, Wf_scales, 
         ctx.enter_context(tc.manual_schedule())
         keep = ctx.enter_context(tc.tile_pool(name="keep", bufs=1))
         x_pool = ctx.enter_context(tc.tile_pool(name="x", bufs=X_BUFS))
-        fa_pool = ctx.enter_context(tc.tile_pool(name="fa", bufs=4))
         ring3 = ctx.enter_context(tc.tile_pool(name="ring3", bufs=3))
         ring2 = ctx.enter_context(tc.tile_pool(name="ring2", bufs=2))
-        psum = ctx.enter_context(tc.psum_pool(name="psum", bufs=2))
+        psum4 = ctx.enter_context(tc.psum_pool(name="psum4", bufs=4))
+        psum2 = ctx.enter_context(tc.psum_pool(name="psum2", bufs=2))
 
         x_pairs, x_grouped, x_codes, x_scales = {}, {}, {}, {}
-        fa_blocks, fa_grouped, fa_codes, fa_scales, margins = {}, {}, {}, {}, {}
+        fa_blocks, fa_grouped, fa_codes, fa_scales, dots, margins = {}, {}, {}, {}, {}, {}
 
-        def load_pair(pair):
+        def load_pair(pair, pieces=1):
             x_sb = x_pool.tile([P, 2, STATE_DIM], BF16)
-            nc.sync.dma_start(out=x_sb[:], in_=x_rows[:, 2 * pair : 2 * pair + 2, :])
+            step = 2 // pieces
+            for i in range(0, 2, step):
+                nc.sync.dma_start(
+                    out=x_sb[:, i : i + step, :], in_=x_rows[:, 2 * pair + i : 2 * pair + i + step, :]
+                )
             x_pairs[pair] = x_sb
 
-        load_pair(0)
+        load_pair(0, pieces=2)
+        load_pair(1)
 
-        ident_bf16 = keep.tile([P, P], BF16)
-        make_identity(nc, ident_bf16[:])
         ident_f32 = keep.tile([P, P], F32)
         make_identity(nc, ident_f32[:])
+        ident_bf16 = keep.tile([P, P], BF16)
+        make_identity(nc, ident_bf16[:])
 
         w_words = keep.tile([P, K_PASSES, 2 * FEATURES], U8, align_bytes=64)
-        nc.sync.dma_start(out=w_words[:].bitcast(I32), in_=Wf_words.bitcast(I32).rearrange("g p b -> p g b"))
         w_scales = keep.tile([P, K_PASSES, FEATURES], U8, align_bytes=64)
         nc.vector.memset(w_scales[:].bitcast(I32), 0)
         for quadrant in range(4):
@@ -72,14 +71,17 @@ def tile_curiositymodule_pa_t_kernel(tc, next_state, seen, Wf_words, Wf_scales, 
                 out=w_scales[32 * quadrant : 32 * quadrant + 4].bitcast(I32),
                 in_=Wf_scales[:, 4 * quadrant : 4 * quadrant + 4, :].bitcast(I32).rearrange("g r n -> r g n"),
             )
-        for pair in range(1, X_BUFS - 1):
+        load_pair(2)
+        nc.sync.dma_start(out=w_words[:].bitcast(I32), in_=Wf_words.bitcast(I32).rearrange("g p b -> p g b"))
+        load_pair(3)
+        seen_sb = keep.tile([P, MEMORY_HALVES, FEATURES], BF16)
+        nc.sync.dma_start(out=seen_sb[:], in_=seen.rearrange("(c m) j -> m c j", m=P))
+        for pair in range(4, X_BUFS):
             load_pair(pair)
 
         bias_rows = keep.tile([P, P], BF16)
         nc.vector.memset(bias_rows[:], 0.0)
         nc.scalar.dma_start(out=bias_rows[0:PACK, :], in_=b_feat.rearrange("(t p) -> t p", p=P))
-        seen_sb = keep.tile([P, MEMORY_HALVES, FEATURES], BF16)
-        nc.scalar.dma_start(out=seen_sb[:], in_=seen.rearrange("(c m) j -> m c j", m=P))
 
         one = keep.tile([P, 1], F32)
         nc.vector.memset(one[:], 1.0)
@@ -88,71 +90,77 @@ def tile_curiositymodule_pa_t_kernel(tc, next_state, seen, Wf_words, Wf_scales, 
         seen_grouped = keep.tile([P, MEMORY, PACK], BF16, align_bytes=64)
         seen_codes = keep.tile([P, MEMORY], U32, align_bytes=64)
         seen_scales = keep.tile([P, MEMORY], U8, align_bytes=64)
-        for c in range(MEMORY_HALVES):
-            seen_ps = psum.tile([P, PACK, P], BF16, tag="ft")
-            for t in range(PACK):
-                nc.tensor.transpose(seen_ps[:, t, :], seen_sb[:, c, t * P : (t + 1) * P], ident_bf16[:])
-            nc.vector.tensor_copy(
-                out=seen_grouped[:, c * P : (c + 1) * P, :], in_=seen_ps[:].rearrange("p t m -> p m t")
-            )
-        nc.vector.quantize_mx(
-            out=seen_codes[:].bitcast(FP8X4), scales=seen_scales[:], in_=seen_grouped[:].rearrange("p m t -> p (m t)")
-        )
-
-        s2 = keep.tile([P, MEMORY_HALVES], F32)
-        for c in range(MEMORY_HALVES):
-            seen_squares = ring2.tile([P, FEATURES], F32)
-            nc.scalar.activation(
-                out=seen_squares[:], in_=seen_sb[:, c, :], func=ACT.Square, accum_out=s2[:, c : c + 1]
-            )
         half_s2 = keep.tile([P, MEMORY], F32)
+        s2 = keep.tile([P, MEMORY_HALVES], F32)
+        s2_repeated = keep.tile([P, MEMORY_HALVES, P], F32)
         bias = keep.tile([P, PACK], F32)
 
-        def turn_small_vectors():
-            bias_ps = psum.tile([P, P], BF16, tag="dot")
+        def prepare_bias():
+            bias_ps = psum4.tile([P, P], BF16, tag="feat")
             nc.tensor.transpose(bias_ps[:], bias_rows[:], ident_bf16[:])
             nc.vector.tensor_copy(out=bias[:], in_=bias_ps[:, 0:PACK])
-            s2_ps = psum.tile([P, MEMORY_HALVES, P], F32, tag="dot")
+
+        def transpose_memory():
             for c in range(MEMORY_HALVES):
-                s2_repeated = ring2.tile([P, P], F32)
-                nc.vector.tensor_copy(out=s2_repeated[:], in_=s2[:, c : c + 1].to_broadcast([P, P]))
-                nc.tensor.transpose(s2_ps[:, c, :], s2_repeated[:], ident_f32[:])
+                seen_ps = psum4.tile([P, PACK, P], BF16, tag="feat")
+                for t in range(PACK):
+                    nc.tensor.transpose(seen_ps[:, t, :], seen_sb[:, c, t * P : (t + 1) * P], ident_bf16[:])
+                nc.vector.tensor_copy(
+                    out=seen_grouped[:, c * P : (c + 1) * P, :], in_=seen_ps[:].rearrange("p t m -> p m t")
+                )
+                seen_squares = ring2.tile([P, FEATURES], F32)
+                nc.scalar.activation(
+                    out=seen_squares[:], in_=seen_sb[:, c, :], func=ACT.Square, accum_out=s2[:, c : c + 1]
+                )
+
+        def quantise_memory():
+            nc.vector.quantize_mx(
+                out=seen_codes[:].bitcast(FP8X4),
+                scales=seen_scales[:],
+                in_=seen_grouped[:].rearrange("p m t -> p (m t)"),
+            )
+            for c in range(MEMORY_HALVES):
+                nc.vector.tensor_copy(out=s2_repeated[:, c, :], in_=s2[:, c : c + 1].to_broadcast([P, P]))
+
+        def turn_memory_norms():
+            s2_ps = psum4.tile([P, MEMORY_HALVES, P], F32, tag="feat")
+            for c in range(MEMORY_HALVES):
+                nc.tensor.transpose(s2_ps[:, c, :], s2_repeated[:, c, :], ident_f32[:])
             nc.vector.tensor_scalar_mul(out=half_s2[:], in0=s2_ps[:].rearrange("p c m -> p (c m)"), scalar1=0.5)
 
         a2 = keep.tile([P, GROUPS], F32)
         best = keep.tile([P, GROUPS], F32)
 
-        def transpose_states(pair):
-            grouped = ring3.tile([P, K_PASSES, PAIR_STATES, 2], F32, name="x_grouped", align_bytes=64)
-            x_grouped[pair] = grouped
-            for i in range(2):
-                words = x_pairs[pair][:, i, :].bitcast(F32)
-                xt = psum.tile([P, K_PASSES, 2, P], F32)
-                for g in range(K_PASSES):
-                    for u in range(2):
-                        nc.tensor.transpose(xt[:, g, u, :], words[:, 256 * g + u : 256 * (g + 1) : 2], ident_f32[:])
-                copy = nc.vector.tensor_copy if i == 0 else nc.scalar.copy
-                copy(out=grouped[:, :, i * P : (i + 1) * P, :], in_=xt[:].rearrange("p g u s -> p g s u"))
-
-        def quantise_states(pair):
-            block, half = pair // 2, pair % 2
-            if half == 0:
-                codes = ring3.tile([P, K_PASSES, BLOCK_STATES], U32, name="x_codes", align_bytes=64)
-                scales = ring3.tile([P, K_PASSES, BLOCK_STATES], U8, name="x_scales", align_bytes=64)
-                x_codes[block], x_scales[block] = codes, scales
-            cols = slice(half * PAIR_STATES, (half + 1) * PAIR_STATES)
+        def transpose_group(block, i):
+            if i == 0:
+                grouped = ring2.tile([P, K_PASSES, BLOCK_STATES, 2], F32, name="x_grouped", align_bytes=64)
+                x_grouped[block] = grouped
+            words = x_pairs[2 * block + i // 2][:, i % 2, :].bitcast(F32)
+            xt = psum2.tile([P, K_PASSES, 2, P], F32)
             for g in range(K_PASSES):
-                nc.vector.quantize_mx(
-                    out=x_codes[block][:, g, cols].bitcast(FP8X4),
-                    scales=x_scales[block][:, g, cols],
-                    in_=x_grouped[pair][:, g].rearrange("p s u -> p (s u)").bitcast(BF16),
-                )
+                for u in range(2):
+                    nc.tensor.transpose(xt[:, g, u, :], words[:, 256 * g + u : 256 * (g + 1) : 2], ident_f32[:])
+            on_vector = i >= 2 if block == 1 else i % 2 == 0
+            copy = nc.vector.tensor_copy if on_vector else nc.scalar.copy
+            copy(
+                out=x_grouped[block][:, :, i * P : (i + 1) * P, :], in_=xt[:].rearrange("p g u s -> p g s u")
+            )
+
+        def quantise_states(block):
+            codes = ring2.tile([P, K_PASSES, BLOCK_STATES], U32, name="x_codes", align_bytes=64)
+            scales = ring2.tile([P, K_PASSES, BLOCK_STATES], U8, name="x_scales", align_bytes=64)
+            nc.vector.quantize_mx(
+                out=codes[:].rearrange("p g s -> p (g s)").bitcast(FP8X4),
+                scales=scales[:].rearrange("p g s -> p (g s)"),
+                in_=x_grouped[block][:].rearrange("p g s u -> p (g s u)").bitcast(BF16),
+            )
+            x_codes[block], x_scales[block] = codes, scales
 
         def features(block, t):
             if t == 0:
-                fa = fa_pool.tile([P, PACK, BLOCK_STATES], F32)
+                fa = ring3.tile([P, PACK, BLOCK_STATES], F32)
                 fa_blocks[block] = fa
-            z = psum.tile([P, BLOCK_STATES], F32)
+            z = psum4.tile([P, BLOCK_STATES], F32, tag="feat")
             for g in range(K_PASSES):
                 nc.tensor.matmul_mx(
                     out=z[:],
@@ -167,7 +175,7 @@ def tile_curiositymodule_pa_t_kernel(tc, next_state, seen, Wf_words, Wf_scales, 
 
         def regroup_features(pair):
             cols = slice((pair % 2) * PAIR_STATES, (pair % 2 + 1) * PAIR_STATES)
-            grouped = keep.tile([P, PAIR_STATES, PACK], BF16, name="fa_grouped", align_bytes=64)
+            grouped = ring2.tile([P, PAIR_STATES, PACK], BF16, name="fa_grouped", align_bytes=64)
             nc.gpsimd.tensor_scalar(
                 out=grouped[:],
                 in0=fa_blocks[pair // 2][:, :, cols].rearrange("p t s -> p s t"),
@@ -186,22 +194,21 @@ def tile_curiositymodule_pa_t_kernel(tc, next_state, seen, Wf_words, Wf_scales, 
             )
             fa_codes[pair], fa_scales[pair] = codes, scales
 
-        def square_norms(pair):
-            for i in range(2):
-                cols = slice((2 * (pair % 2) + i) * P, (2 * (pair % 2) + i + 1) * P)
-                ft = psum.tile([P, PACK, P], F32)
-                for t in range(PACK):
-                    nc.tensor.transpose(ft[:, t, :], fa_blocks[pair // 2][:, t, cols], ident_f32[:])
-                squares = ring2.tile([P, FEATURES], F32)
-                nc.scalar.activation(
-                    out=squares[:],
-                    in_=ft[:].rearrange("p t f -> p (t f)"),
-                    func=ACT.Square,
-                    accum_out=a2[:, 2 * pair + i : 2 * pair + i + 1],
-                )
+        def square_norms(block, i):
+            ft = psum4.tile([P, PACK, P], F32, tag="feat")
+            for t in range(PACK):
+                nc.tensor.transpose(ft[:, t, :], fa_blocks[block][:, t, i * P : (i + 1) * P], ident_f32[:])
+            squares = ring2.tile([P, FEATURES], F32)
+            group = BLOCK_GROUPS * block + i
+            nc.scalar.activation(
+                out=squares[:],
+                in_=ft[:].rearrange("p t f -> p (t f)"),
+                func=ACT.Square,
+                accum_out=a2[:, group : group + 1],
+            )
 
         def distances(pair):
-            dot = psum.tile([P, 2, MEMORY], F32)
+            dot = psum2.tile([P, 2, MEMORY], F32)
             for i in range(2):
                 nc.tensor.matmul_mx(
                     out=dot[:, i, :],
@@ -212,9 +219,15 @@ def tile_curiositymodule_pa_t_kernel(tc, next_state, seen, Wf_words, Wf_scales, 
                     start=True,
                     stop=True,
                 )
+            dots[pair] = dot
+
+        def subtract_norms(pair):
             margin = ring2.tile([P, 2, MEMORY], F32)
             nc.vector.tensor_tensor(
-                out=margin[:], in0=dot[:], in1=half_s2[:].unsqueeze(1).to_broadcast([P, 2, MEMORY]), op=ALU.subtract
+                out=margin[:],
+                in0=dots[pair][:],
+                in1=half_s2[:].unsqueeze(1).to_broadcast([P, 2, MEMORY]),
+                op=ALU.subtract,
             )
             margins[pair] = margin
 
@@ -223,34 +236,47 @@ def tile_curiositymodule_pa_t_kernel(tc, next_state, seen, Wf_words, Wf_scales, 
                 out=best[:, 2 * pair : 2 * pair + 2], in_=margins[pair][:], axis=mybir.AxisListType.X, op=ALU.max
             )
 
-        def is_pair(pair):
-            return 0 <= pair < PAIRS
-
         def pipeline_step(step):
-            if is_pair(step + TRANSPOSE_LEAD + X_BUFS - 1):
-                load_pair(step + TRANSPOSE_LEAD + X_BUFS - 1)
-            if is_pair(step + TRANSPOSE_LEAD):
-                transpose_states(step + TRANSPOSE_LEAD)
-            if is_pair(step - NORM_LAG):
-                square_norms(step - NORM_LAG)
-            if is_pair(step - BEST_LAG):
-                nearest(step - BEST_LAG)
-            if is_pair(step + QUANTISE_LEAD):
-                quantise_states(step + QUANTISE_LEAD)
-            if is_pair(step - QUANTISE_LAG):
-                quantise_features(step - QUANTISE_LAG)
-            if is_pair(step - REGROUP_LAG):
-                regroup_features(step - REGROUP_LAG)
-            if is_pair(step):
-                features(step // 2, 2 * (step % 2))
-                features(step // 2, 2 * (step % 2) + 1)
-            if is_pair(step - DISTANCE_LAG):
-                distances(step - DISTANCE_LAG)
+            new, now, old, done = step + 1, step, step - 1, step - 2
+            for pair in (2 * new + X_BUFS - 2, 2 * new + X_BUFS - 1):
+                if step >= 0 and pair < PAIRS:
+                    load_pair(pair)
+            if 0 <= old < BLOCKS:
+                regroup_features(2 * old)
+                regroup_features(2 * old + 1)
+            if 0 <= done < BLOCKS:
+                subtract_norms(2 * done)
+            for i in range(BLOCK_GROUPS):
+                if new < BLOCKS:
+                    transpose_group(new, i)
+                if 0 <= old < BLOCKS:
+                    square_norms(old, i)
+                if 0 <= done < BLOCKS and i == 0:
+                    subtract_norms(2 * done + 1)
+                    nearest(2 * done)
+            if 0 <= done < BLOCKS:
+                nearest(2 * done + 1)
+            if step == -1:
+                prepare_bias()
+            if step == 0:
+                transpose_memory()
+            if step == 1:
+                turn_memory_norms()
+            if 0 <= old < BLOCKS:
+                quantise_features(2 * old)
+                quantise_features(2 * old + 1)
+            if new < BLOCKS:
+                quantise_states(new)
+            if step == 0:
+                quantise_memory()
+            if 0 <= now < BLOCKS:
+                for t in range(PACK):
+                    features(now, t)
+            if 0 <= old < BLOCKS:
+                distances(2 * old)
+                distances(2 * old + 1)
 
-        for step in range(-TRANSPOSE_LEAD, 0):
-            pipeline_step(step)
-        turn_small_vectors()
-        for step in range(0, PAIRS + max(BEST_LAG, NORM_LAG)):
+        for step in range(-1, BLOCKS + 2):
             pipeline_step(step)
 
         d2 = keep.tile([P, GROUPS], F32)

@@ -25,6 +25,7 @@ MEMORY_HALVES = MEMORY // P
 BLOCK_GROUPS = 4
 BLOCKS = GROUPS // BLOCK_GROUPS
 X_BUFS = 8
+NORM_LAG = 4
 SQRT_FLOOR = 1e-30
 
 FLOPS = 2 * STATES * STATE_DIM * FEATURES + 2 * STATES * FEATURES * MEMORY
@@ -38,6 +39,7 @@ def tile_curiositymodule_pa_t_kernel(tc, next_state, seen, Wf_words, Wf_scales, 
         ctx.enter_context(tc.manual_schedule())
         keep = ctx.enter_context(tc.tile_pool(name="keep", bufs=1))
         x_pool = ctx.enter_context(tc.tile_pool(name="x", bufs=X_BUFS))
+        fa_pool = ctx.enter_context(tc.tile_pool(name="fa", bufs=5))
         ring3 = ctx.enter_context(tc.tile_pool(name="ring3", bufs=3))
         ring2 = ctx.enter_context(tc.tile_pool(name="ring2", bufs=2))
         psum4 = ctx.enter_context(tc.psum_pool(name="psum4", bufs=4))
@@ -112,6 +114,8 @@ def tile_curiositymodule_pa_t_kernel(tc, next_state, seen, Wf_words, Wf_scales, 
                 nc.scalar.activation(
                     out=seen_squares[:], in_=seen_sb[:, c, :], func=ACT.Square, accum_out=s2[:, c : c + 1]
                 )
+            for c in range(MEMORY_HALVES):
+                nc.vector.tensor_copy(out=s2_repeated[:, c, :], in_=s2[:, c : c + 1].to_broadcast([P, P]))
 
         def quantise_memory():
             nc.vector.quantize_mx(
@@ -119,8 +123,6 @@ def tile_curiositymodule_pa_t_kernel(tc, next_state, seen, Wf_words, Wf_scales, 
                 scales=seen_scales[:],
                 in_=seen_grouped[:].rearrange("p m t -> p (m t)"),
             )
-            for c in range(MEMORY_HALVES):
-                nc.vector.tensor_copy(out=s2_repeated[:, c, :], in_=s2[:, c : c + 1].to_broadcast([P, P]))
 
         def turn_memory_norms():
             s2_ps = psum4.tile([P, MEMORY_HALVES, P], F32, tag="feat")
@@ -158,7 +160,7 @@ def tile_curiositymodule_pa_t_kernel(tc, next_state, seen, Wf_words, Wf_scales, 
 
         def features(block, t):
             if t == 0:
-                fa = ring3.tile([P, PACK, BLOCK_STATES], F32)
+                fa = fa_pool.tile([P, PACK, BLOCK_STATES], F32)
                 fa_blocks[block] = fa
             z = psum4.tile([P, BLOCK_STATES], F32, tag="feat")
             for g in range(K_PASSES):
@@ -175,15 +177,14 @@ def tile_curiositymodule_pa_t_kernel(tc, next_state, seen, Wf_words, Wf_scales, 
 
         def regroup_features(pair):
             cols = slice((pair % 2) * PAIR_STATES, (pair % 2 + 1) * PAIR_STATES)
+            by_state = fa_blocks[pair // 2][:, :, cols].rearrange("p t s -> p s t")
             grouped = ring2.tile([P, PAIR_STATES, PACK], BF16, name="fa_grouped", align_bytes=64)
-            nc.gpsimd.tensor_scalar(
-                out=grouped[:],
-                in0=fa_blocks[pair // 2][:, :, cols].rearrange("p t s -> p s t"),
-                scalar1=1.0,
-                scalar2=0.0,
-                op0=ALU.mult,
-                op1=ALU.add,
-            )
+            if pair == PAIRS - 1:
+                nc.scalar.copy(out=grouped[:], in_=by_state)
+            else:
+                nc.gpsimd.tensor_scalar(
+                    out=grouped[:], in0=by_state, scalar1=1.0, scalar2=0.0, op0=ALU.mult, op1=ALU.add
+                )
             fa_grouped[pair] = grouped
 
         def quantise_features(pair):
@@ -194,18 +195,19 @@ def tile_curiositymodule_pa_t_kernel(tc, next_state, seen, Wf_words, Wf_scales, 
             )
             fa_codes[pair], fa_scales[pair] = codes, scales
 
-        def square_norms(block, i):
-            ft = psum4.tile([P, PACK, P], F32, tag="feat")
-            for t in range(PACK):
-                nc.tensor.transpose(ft[:, t, :], fa_blocks[block][:, t, i * P : (i + 1) * P], ident_f32[:])
-            squares = ring2.tile([P, FEATURES], F32)
-            group = BLOCK_GROUPS * block + i
-            nc.scalar.activation(
-                out=squares[:],
-                in_=ft[:].rearrange("p t f -> p (t f)"),
-                func=ACT.Square,
-                accum_out=a2[:, group : group + 1],
-            )
+        def square_norms(pair):
+            for i in range(2):
+                cols = slice((2 * (pair % 2) + i) * P, (2 * (pair % 2) + i + 1) * P)
+                ft = psum4.tile([P, PACK, P], F32, tag="feat")
+                for t in range(PACK):
+                    nc.tensor.transpose(ft[:, t, :], fa_blocks[pair // 2][:, t, cols], ident_f32[:])
+                squares = ring2.tile([P, FEATURES], F32)
+                nc.scalar.activation(
+                    out=squares[:],
+                    in_=ft[:].rearrange("p t f -> p (t f)"),
+                    func=ACT.Square,
+                    accum_out=a2[:, 2 * pair + i : 2 * pair + i + 1],
+                )
 
         def distances(pair):
             dot = psum2.tile([P, 2, MEMORY], F32)
@@ -236,48 +238,69 @@ def tile_curiositymodule_pa_t_kernel(tc, next_state, seen, Wf_words, Wf_scales, 
                 out=best[:, 2 * pair : 2 * pair + 2], in_=margins[pair][:], axis=mybir.AxisListType.X, op=ALU.max
             )
 
+        def is_pair(pair):
+            return 0 <= pair < PAIRS
+
         def pipeline_step(step):
             new, now, old, done = step + 1, step, step - 1, step - 2
-            for pair in (2 * new + X_BUFS - 2, 2 * new + X_BUFS - 1):
-                if step >= 0 and pair < PAIRS:
-                    load_pair(pair)
-            if 0 <= old < BLOCKS:
-                regroup_features(2 * old)
-                regroup_features(2 * old + 1)
-            if 0 <= done < BLOCKS:
-                subtract_norms(2 * done)
-            for i in range(BLOCK_GROUPS):
-                if new < BLOCKS:
-                    transpose_group(new, i)
+            for half in range(2):
+                if step >= 0 and 2 * new + X_BUFS - 2 + half < PAIRS:
+                    load_pair(2 * new + X_BUFS - 2 + half)
                 if 0 <= old < BLOCKS:
-                    square_norms(old, i)
-                if 0 <= done < BLOCKS and i == 0:
+                    regroup_features(2 * old + half)
+                if half == 0 and 0 <= done < BLOCKS:
+                    subtract_norms(2 * done)
+                for i in range(2):
+                    if new < BLOCKS:
+                        transpose_group(new, 2 * half + i)
+                if half == 0 and 0 <= done < BLOCKS:
                     subtract_norms(2 * done + 1)
                     nearest(2 * done)
-            if 0 <= done < BLOCKS:
-                nearest(2 * done + 1)
-            if step == -1:
-                prepare_bias()
-            if step == 0:
-                transpose_memory()
-            if step == 1:
-                turn_memory_norms()
-            if 0 <= old < BLOCKS:
-                quantise_features(2 * old)
-                quantise_features(2 * old + 1)
-            if new < BLOCKS:
-                quantise_states(new)
-            if step == 0:
-                quantise_memory()
-            if 0 <= now < BLOCKS:
-                for t in range(PACK):
-                    features(now, t)
+                    nearest(2 * done + 1)
+                if is_pair(2 * step + half - NORM_LAG):
+                    square_norms(2 * step + half - NORM_LAG)
+                if step == -1 and half == 0:
+                    prepare_bias()
+                if step == 0 and half == 1:
+                    transpose_memory()
+                if step == 1 and half == 1:
+                    turn_memory_norms()
+                if half == 1:
+                    if step == 1:
+                        quantise_memory()
+                    if 0 <= old < BLOCKS:
+                        quantise_features(2 * old)
+                        quantise_features(2 * old + 1)
+                    if new < BLOCKS:
+                        quantise_states(new)
+                if 0 <= now < BLOCKS:
+                    features(now, 2 * half)
+                    features(now, 2 * half + 1)
             if 0 <= old < BLOCKS:
                 distances(2 * old)
                 distances(2 * old + 1)
 
-        for step in range(-1, BLOCKS + 2):
+        for step in range(-1, BLOCKS):
             pipeline_step(step)
+
+        regroup_features(PAIRS - 2)
+        regroup_features(PAIRS - 1)
+        for pair in (PAIRS - 4, PAIRS - 3):
+            subtract_norms(pair)
+        for pair in (PAIRS - 4, PAIRS - 3):
+            nearest(pair)
+        for pair in range(PAIRS - NORM_LAG, PAIRS - NORM_LAG + 2):
+            square_norms(pair)
+        for pair in (PAIRS - 2, PAIRS - 1):
+            quantise_features(pair)
+        for pair in (PAIRS - 2, PAIRS - 1):
+            distances(pair)
+        for pair in (PAIRS - 2, PAIRS - 1):
+            subtract_norms(pair)
+        for pair in (PAIRS - 2, PAIRS - 1):
+            nearest(pair)
+        for pair in range(PAIRS - NORM_LAG + 2, PAIRS):
+            square_norms(pair)
 
         d2 = keep.tile([P, GROUPS], F32)
         nc.vector.scalar_tensor_tensor(out=d2[:], in0=best[:], scalar=-2.0, in1=a2[:], op0=ALU.mult, op1=ALU.add)

@@ -26,6 +26,7 @@ BLOCK_GROUPS = 4
 BLOCKS = GROUPS // BLOCK_GROUPS
 X_BUFS = 8
 NORM_LAG = 4
+SORTED = (0, 2)
 SQRT_FLOOR = 1e-30
 
 FLOPS = 2 * STATES * STATE_DIM * FEATURES + 2 * STATES * FEATURES * MEMORY
@@ -45,7 +46,8 @@ def tile_curiositymodule_pa_t_kernel(tc, next_state, seen, Wf_words, Wf_scales, 
         psum4 = ctx.enter_context(tc.psum_pool(name="psum4", bufs=4))
         psum2 = ctx.enter_context(tc.psum_pool(name="psum2", bufs=2))
 
-        x_pairs, x_grouped, x_codes, x_scales = {}, {}, {}, {}
+        ring4 = ctx.enter_context(tc.tile_pool(name="ring4", bufs=4))
+        x_pairs, x_sorted, x_grouped, x_codes, x_scales = {}, {}, {}, {}, {}
         fa_blocks, fa_grouped, fa_codes, fa_scales, dots, margins = {}, {}, {}, {}, {}, {}
 
         def load_pair(pair, pieces=1):
@@ -133,6 +135,12 @@ def tile_curiositymodule_pa_t_kernel(tc, next_state, seen, Wf_words, Wf_scales, 
         a2 = keep.tile([P, GROUPS], F32)
         best = keep.tile([P, GROUPS], F32)
 
+        def sort_words(block, i):
+            sorted_words = ring4.tile([P, K_PASSES, 2, P], F32)
+            words = x_pairs[2 * block + i // 2][:, i % 2, :].bitcast(F32)
+            nc.vector.tensor_copy(out=sorted_words[:], in_=words.rearrange("q (g p u) -> q g u p", g=K_PASSES, u=2))
+            x_sorted[block, i] = sorted_words
+
         def transpose_group(block, i):
             if i == 0:
                 grouped = ring2.tile([P, K_PASSES, BLOCK_STATES, 2], F32, name="x_grouped", align_bytes=64)
@@ -141,7 +149,11 @@ def tile_curiositymodule_pa_t_kernel(tc, next_state, seen, Wf_words, Wf_scales, 
             xt = psum2.tile([P, K_PASSES, 2, P], F32)
             for g in range(K_PASSES):
                 for u in range(2):
-                    nc.tensor.transpose(xt[:, g, u, :], words[:, 256 * g + u : 256 * (g + 1) : 2], ident_f32[:])
+                    if (block, i) in x_sorted:
+                        in_ = x_sorted[block, i][:, g, u, :]
+                    else:
+                        in_ = words[:, 256 * g + u : 256 * (g + 1) : 2]
+                    nc.tensor.transpose(xt[:, g, u, :], in_, ident_f32[:])
             on_vector = i >= 2 if block == 1 else i % 2 == 0
             copy = nc.vector.tensor_copy if on_vector else nc.scalar.copy
             copy(
@@ -266,6 +278,9 @@ def tile_curiositymodule_pa_t_kernel(tc, next_state, seen, Wf_words, Wf_scales, 
                 if step == 1 and half == 1:
                     turn_memory_norms()
                 if half == 1:
+                    if 2 <= new + 1 < BLOCKS:
+                        for i in SORTED:
+                            sort_words(new + 1, i)
                     if step == 1:
                         quantise_memory()
                     if 0 <= old < BLOCKS:

@@ -25,8 +25,9 @@ MEMORY_HALVES = MEMORY // P
 BLOCK_GROUPS = 4
 BLOCKS = GROUPS // BLOCK_GROUPS
 X_BUFS = 8
-NORM_LAG = 4
-SORTED = (0, 2)
+NORM_LAG = 3
+SORTED = (2,)
+FIRST_SORTED = 4
 SQRT_FLOOR = 1e-30
 
 FLOPS = 2 * STATES * STATE_DIM * FEATURES + 2 * STATES * FEATURES * MEMORY
@@ -46,7 +47,6 @@ def tile_curiositymodule_pa_t_kernel(tc, next_state, seen, Wf_words, Wf_scales, 
         psum4 = ctx.enter_context(tc.psum_pool(name="psum4", bufs=4))
         psum2 = ctx.enter_context(tc.psum_pool(name="psum2", bufs=2))
 
-        ring4 = ctx.enter_context(tc.tile_pool(name="ring4", bufs=4))
         x_pairs, x_sorted, x_grouped, x_codes, x_scales = {}, {}, {}, {}, {}
         fa_blocks, fa_grouped, fa_codes, fa_scales, dots, margins = {}, {}, {}, {}, {}, {}
 
@@ -136,7 +136,7 @@ def tile_curiositymodule_pa_t_kernel(tc, next_state, seen, Wf_words, Wf_scales, 
         best = keep.tile([P, GROUPS], F32)
 
         def sort_words(block, i):
-            sorted_words = ring4.tile([P, K_PASSES, 2, P], F32)
+            sorted_words = ring3.tile([P, K_PASSES, 2, P], F32)
             words = x_pairs[2 * block + i // 2][:, i % 2, :].bitcast(F32)
             nc.vector.tensor_copy(out=sorted_words[:], in_=words.rearrange("q (g p u) -> q g u p", g=K_PASSES, u=2))
             x_sorted[block, i] = sorted_words
@@ -169,6 +169,19 @@ def tile_curiositymodule_pa_t_kernel(tc, next_state, seen, Wf_words, Wf_scales, 
                 in_=x_grouped[block][:].rearrange("p g s u -> p (g s u)").bitcast(BF16),
             )
             x_codes[block], x_scales[block] = codes, scales
+
+        def quantise_pair(block, half):
+            if half == 0:
+                codes = ring2.tile([P, K_PASSES, BLOCK_STATES], U32, name="x_codes", align_bytes=64)
+                scales = ring2.tile([P, K_PASSES, BLOCK_STATES], U8, name="x_scales", align_bytes=64)
+                x_codes[block], x_scales[block] = codes, scales
+            states = slice(half * PAIR_STATES, (half + 1) * PAIR_STATES)
+            for g in range(K_PASSES):
+                nc.vector.quantize_mx(
+                    out=x_codes[block][:, g, states].bitcast(FP8X4),
+                    scales=x_scales[block][:, g, states],
+                    in_=x_grouped[block][:, g, states, :].rearrange("p s u -> p (s u)").bitcast(BF16),
+                )
 
         def features(block, t):
             if t == 0:
@@ -278,7 +291,7 @@ def tile_curiositymodule_pa_t_kernel(tc, next_state, seen, Wf_words, Wf_scales, 
                 if step == 1 and half == 1:
                     turn_memory_norms()
                 if half == 1:
-                    if 2 <= new + 1 < BLOCKS:
+                    if FIRST_SORTED <= new + 1 < BLOCKS:
                         for i in SORTED:
                             sort_words(new + 1, i)
                     if step == 1:
@@ -286,8 +299,10 @@ def tile_curiositymodule_pa_t_kernel(tc, next_state, seen, Wf_words, Wf_scales, 
                     if 0 <= old < BLOCKS:
                         quantise_features(2 * old)
                         quantise_features(2 * old + 1)
-                    if new < BLOCKS:
+                    if 0 < new < BLOCKS:
                         quantise_states(new)
+                if new == 0:
+                    quantise_pair(new, half)
                 if 0 <= now < BLOCKS:
                     features(now, 2 * half)
                     features(now, 2 * half + 1)
@@ -302,12 +317,12 @@ def tile_curiositymodule_pa_t_kernel(tc, next_state, seen, Wf_words, Wf_scales, 
         regroup_features(PAIRS - 1)
         for pair in (PAIRS - 4, PAIRS - 3):
             subtract_norms(pair)
-        for pair in (PAIRS - 4, PAIRS - 3):
-            nearest(pair)
+        nearest(PAIRS - 4)
         for pair in range(PAIRS - NORM_LAG, PAIRS - NORM_LAG + 2):
             square_norms(pair)
         for pair in (PAIRS - 2, PAIRS - 1):
             quantise_features(pair)
+        nearest(PAIRS - 3)
         for pair in (PAIRS - 2, PAIRS - 1):
             distances(pair)
         for pair in (PAIRS - 2, PAIRS - 1):
@@ -319,8 +334,7 @@ def tile_curiositymodule_pa_t_kernel(tc, next_state, seen, Wf_words, Wf_scales, 
 
         d2 = keep.tile([P, GROUPS], F32)
         nc.vector.scalar_tensor_tensor(out=d2[:], in0=best[:], scalar=-2.0, in1=a2[:], op0=ALU.mult, op1=ALU.add)
-        nc.vector.tensor_scalar_max(out=d2[:], in0=d2[:], scalar1=SQRT_FLOOR)
+        nc.vector.tensor_scalar(out=d2[:], in0=d2[:], scalar1=SQRT_FLOOR, scalar2=100.0, op0=ALU.max, op1=ALU.min)
         novelty = keep.tile([P, GROUPS], F32)
-        nc.scalar.activation(out=novelty[:], in_=d2[:], func=ACT.Sqrt)
-        nc.vector.tensor_scalar(out=novelty[:], in0=novelty[:], scalar1=0.1, scalar2=1.0, op0=ALU.mult, op1=ALU.min)
-        nc.sync.dma_start(out=out.rearrange("(p c) -> p c", c=GROUPS), in_=novelty[:])
+        nc.scalar.activation(out=novelty[:], in_=d2[:], func=ACT.Sqrt, scale=0.01)
+        nc.scalar.dma_start(out=out.rearrange("(p c) -> p c", c=GROUPS), in_=novelty[:])

@@ -26,8 +26,6 @@ BLOCK_GROUPS = 4
 BLOCKS = GROUPS // BLOCK_GROUPS
 X_BUFS = 8
 NORM_LAG = 3
-SORTED = (2,)
-FIRST_SORTED = 4
 SQRT_FLOOR = 1e-30
 
 FLOPS = 2 * STATES * STATE_DIM * FEATURES + 2 * STATES * FEATURES * MEMORY
@@ -47,7 +45,7 @@ def tile_curiositymodule_pa_t_kernel(tc, next_state, seen, Wf_words, Wf_scales, 
         psum4 = ctx.enter_context(tc.psum_pool(name="psum4", bufs=4))
         psum2 = ctx.enter_context(tc.psum_pool(name="psum2", bufs=2))
 
-        x_pairs, x_sorted, x_grouped, x_codes, x_scales = {}, {}, {}, {}, {}
+        x_pairs, x_grouped, x_codes, x_scales = {}, {}, {}, {}
         fa_blocks, fa_grouped, fa_codes, fa_scales, dots, margins = {}, {}, {}, {}, {}, {}
 
         def load_pair(pair, pieces=1):
@@ -135,12 +133,6 @@ def tile_curiositymodule_pa_t_kernel(tc, next_state, seen, Wf_words, Wf_scales, 
         a2 = keep.tile([P, GROUPS], F32)
         best = keep.tile([P, GROUPS], F32)
 
-        def sort_words(block, i):
-            sorted_words = ring3.tile([P, K_PASSES, 2, P], F32)
-            words = x_pairs[2 * block + i // 2][:, i % 2, :].bitcast(F32)
-            nc.vector.tensor_copy(out=sorted_words[:], in_=words.rearrange("q (g p u) -> q g u p", g=K_PASSES, u=2))
-            x_sorted[block, i] = sorted_words
-
         def transpose_group(block, i):
             if i == 0:
                 grouped = ring2.tile([P, K_PASSES, BLOCK_STATES, 2], F32, name="x_grouped", align_bytes=64)
@@ -149,12 +141,8 @@ def tile_curiositymodule_pa_t_kernel(tc, next_state, seen, Wf_words, Wf_scales, 
             xt = psum2.tile([P, K_PASSES, 2, P], F32)
             for g in range(K_PASSES):
                 for u in range(2):
-                    if (block, i) in x_sorted:
-                        in_ = x_sorted[block, i][:, g, u, :]
-                    else:
-                        in_ = words[:, 256 * g + u : 256 * (g + 1) : 2]
-                    nc.tensor.transpose(xt[:, g, u, :], in_, ident_f32[:])
-            on_vector = i >= 2 if block == 1 else i % 2 == 0
+                    nc.tensor.transpose(xt[:, g, u, :], words[:, 256 * g + u : 256 * (g + 1) : 2], ident_f32[:])
+            on_vector = i >= 2 if block == 1 else i > 0
             copy = nc.vector.tensor_copy if on_vector else nc.scalar.copy
             copy(
                 out=x_grouped[block][:, :, i * P : (i + 1) * P, :], in_=xt[:].rearrange("p g u s -> p g s u")
@@ -291,9 +279,6 @@ def tile_curiositymodule_pa_t_kernel(tc, next_state, seen, Wf_words, Wf_scales, 
                 if step == 1 and half == 1:
                     turn_memory_norms()
                 if half == 1:
-                    if FIRST_SORTED <= new + 1 < BLOCKS:
-                        for i in SORTED:
-                            sort_words(new + 1, i)
                     if step == 1:
                         quantise_memory()
                     if 0 <= old < BLOCKS:

@@ -25,7 +25,7 @@ MEMORY_HALVES = MEMORY // P
 BLOCK_GROUPS = 4
 BLOCKS = GROUPS // BLOCK_GROUPS
 X_BUFS = 8
-NORM_LAG = 3
+NORM_LAG = 2
 SQRT_FLOOR = 1e-30
 
 FLOPS = 2 * STATES * STATE_DIM * FEATURES + 2 * STATES * FEATURES * MEMORY
@@ -64,6 +64,12 @@ def tile_curiositymodule_pa_t_kernel(tc, next_state, seen, Wf_words, Wf_scales, 
         make_identity(nc, ident_f32[:])
         ident_bf16 = keep.tile([P, P], BF16)
         make_identity(nc, ident_bf16[:])
+
+        zeros = keep.tile([P, PAIR_STATES], BF16)
+        nc.vector.memset(zeros[:], 0.0)
+        for i in range(6):
+            warm_up = psum2.tile([P, PAIR_STATES], F32, tag="dot")
+            nc.tensor.matmul(warm_up[:], zeros[:, 0:P], zeros[:], start=True, stop=True)
 
         w_words = keep.tile([P, K_PASSES, 2 * FEATURES], U8, align_bytes=64)
         w_scales = keep.tile([P, K_PASSES, FEATURES], U8, align_bytes=64)
@@ -188,17 +194,14 @@ def tile_curiositymodule_pa_t_kernel(tc, next_state, seen, Wf_words, Wf_scales, 
                 )
             nc.scalar.activation(out=fa_blocks[block][:, t, :], in_=z[:], func=ACT.Relu, bias=bias[:, t : t + 1])
 
-        def regroup_features(pair):
+        def regroup_features(pair, copy):
             cols = slice((pair % 2) * PAIR_STATES, (pair % 2 + 1) * PAIR_STATES)
-            by_state = fa_blocks[pair // 2][:, :, cols].rearrange("p t s -> p s t")
             grouped = ring2.tile([P, PAIR_STATES, PACK], BF16, name="fa_grouped", align_bytes=64)
-            if pair == PAIRS - 1:
-                nc.scalar.copy(out=grouped[:], in_=by_state)
-            else:
-                nc.gpsimd.tensor_scalar(
-                    out=grouped[:], in0=by_state, scalar1=1.0, scalar2=0.0, op0=ALU.mult, op1=ALU.add
-                )
+            copy(out=grouped[:], in_=fa_blocks[pair // 2][:, :, cols].rearrange("p t s -> p s t"))
             fa_grouped[pair] = grouped
+
+        def gpsimd_copy(out, in_):
+            nc.gpsimd.tensor_scalar(out=out, in0=in_, scalar1=1.0, scalar2=0.0, op0=ALU.mult, op1=ALU.add)
 
         def quantise_features(pair):
             codes = ring3.tile([P, PAIR_STATES], U32, name="fa_codes", align_bytes=64)
@@ -260,7 +263,7 @@ def tile_curiositymodule_pa_t_kernel(tc, next_state, seen, Wf_words, Wf_scales, 
                 if step >= 0 and 2 * new + X_BUFS - 2 + half < PAIRS:
                     load_pair(2 * new + X_BUFS - 2 + half)
                 if 0 <= old < BLOCKS:
-                    regroup_features(2 * old + half)
+                    regroup_features(2 * old + half, gpsimd_copy)
                 if half == 0 and 0 <= done < BLOCKS:
                     subtract_norms(2 * done)
                 for i in range(2):
@@ -295,26 +298,43 @@ def tile_curiositymodule_pa_t_kernel(tc, next_state, seen, Wf_words, Wf_scales, 
                 distances(2 * old)
                 distances(2 * old + 1)
 
-        for step in range(-1, BLOCKS):
+        for step in range(-1, BLOCKS - 1):
             pipeline_step(step)
 
-        regroup_features(PAIRS - 2)
-        regroup_features(PAIRS - 1)
-        for pair in (PAIRS - 4, PAIRS - 3):
+        last = BLOCKS - 1
+        first, second, third, fourth = range(2 * last - 2, 2 * last + 2)
+        regroup_features(first, gpsimd_copy)
+        regroup_features(second, gpsimd_copy)
+        for pair in (first - 2, first - 1):
             subtract_norms(pair)
-        nearest(PAIRS - 4)
-        for pair in range(PAIRS - NORM_LAG, PAIRS - NORM_LAG + 2):
-            square_norms(pair)
-        for pair in (PAIRS - 2, PAIRS - 1):
-            quantise_features(pair)
-        nearest(PAIRS - 3)
-        for pair in (PAIRS - 2, PAIRS - 1):
-            distances(pair)
-        for pair in (PAIRS - 2, PAIRS - 1):
-            subtract_norms(pair)
-        for pair in (PAIRS - 2, PAIRS - 1):
+        for pair in (first - 2, first - 1):
             nearest(pair)
-        for pair in range(PAIRS - NORM_LAG + 2, PAIRS):
+        square_norms(third - NORM_LAG)
+        features(last, 0)
+        features(last, 1)
+        features(last, 2)
+        features(last, 3)
+        quantise_features(first)
+        quantise_features(second)
+        distances(first)
+        distances(second)
+        regroup_features(third, nc.scalar.copy)
+        regroup_features(fourth, gpsimd_copy)
+        square_norms(fourth - NORM_LAG)
+        subtract_norms(first)
+        subtract_norms(second)
+        nearest(first)
+        quantise_features(third)
+        quantise_features(fourth)
+        square_norms(fourth - NORM_LAG + 1)
+        distances(third)
+        distances(fourth)
+        nearest(second)
+        subtract_norms(third)
+        subtract_norms(fourth)
+        nearest(third)
+        nearest(fourth)
+        for pair in range(fourth - NORM_LAG + 2, PAIRS):
             square_norms(pair)
 
         d2 = keep.tile([P, GROUPS], F32)

from contextlib import ExitStack

import concourse.mybir as mybir
from concourse.masks import make_identity

F32 = mybir.dt.float32
BF16 = mybir.dt.bfloat16
I32 = mybir.dt.int32
U32 = mybir.dt.uint32
U8 = mybir.dt.uint8
FP8X4 = mybir.dt.float8_e4m3fn_x4
FP4X4 = mybir.dt.float4_e2m1fn_x4
ACT = mybir.ActivationFunctionType
ALU = mybir.AluOpType

P = 128
PACK = 4
STATES, STATE_DIM, FEATURES, MEMORY = 8192, 1024, 512, 256
K_PASSES = STATE_DIM // (P * PACK)
GROUPS = STATES // P
PAIRS = GROUPS // 2
PAIR_STATES = 2 * P
BLOCK_STATES = 4 * P
MEMORY_HALVES = MEMORY // P
BLOCK_GROUPS = 4
BLOCKS = GROUPS // BLOCK_GROUPS
X_BUFS = 8
NORM_LAG = 2
SQRT_FLOOR = 1e-30

FLOPS = 2 * STATES * STATE_DIM * FEATURES + 2 * STATES * FEATURES * MEMORY


def tile_curiositymodule_pa_t_kernel(tc, next_state, seen, Wf_words, Wf_scales, b_feat, out):
    nc = tc.nc
    x_rows = next_state.rearrange("(p c) k -> p c k", c=GROUPS)

    with ExitStack() as ctx:
        ctx.enter_context(tc.manual_schedule())
        keep = ctx.enter_context(tc.tile_pool(name="keep", bufs=1))
        x_pool = ctx.enter_context(tc.tile_pool(name="x", bufs=X_BUFS))
        fa_pool = ctx.enter_context(tc.tile_pool(name="fa", bufs=5))
        ring3 = ctx.enter_context(tc.tile_pool(name="ring3", bufs=3))
        ring2 = ctx.enter_context(tc.tile_pool(name="ring2", bufs=2))
        psum4 = ctx.enter_context(tc.psum_pool(name="psum4", bufs=4))
        psum2 = ctx.enter_context(tc.psum_pool(name="psum2", bufs=2))

        x_pairs, x_grouped, x_codes, x_scales = {}, {}, {}, {}
        fa_blocks, fa_grouped, fa_codes, fa_scales, dots, margins = {}, {}, {}, {}, {}, {}

        def load_pair(pair, pieces=1):
            x_sb = x_pool.tile([P, 2, STATE_DIM], BF16)
            step = 2 // pieces
            for i in range(0, 2, step):
                nc.sync.dma_start(
                    out=x_sb[:, i : i + step, :], in_=x_rows[:, 2 * pair + i : 2 * pair + i + step, :]
                )
            x_pairs[pair] = x_sb

        load_pair(0, pieces=2)
        load_pair(1)

        ident_f32 = keep.tile([P, P], F32)
        make_identity(nc, ident_f32[:])
        ident_bf16 = keep.tile([P, P], BF16)
        make_identity(nc, ident_bf16[:])

        zeros = keep.tile([P, PAIR_STATES], BF16)
        nc.vector.memset(zeros[:], 0.0)
        for i in range(6):
            warm_up = psum2.tile([P, PAIR_STATES], F32, tag="dot")
            nc.tensor.matmul(warm_up[:], zeros[:, 0:P], zeros[:], start=True, stop=True)

        w_words = keep.tile([P, K_PASSES, 2 * FEATURES], U8, align_bytes=64)
        w_scales = keep.tile([P, K_PASSES, FEATURES], U8, align_bytes=64)
        nc.vector.memset(w_scales[:].bitcast(I32), 0)
        for quadrant in range(4):
            nc.sync.dma_start(
                out=w_scales[32 * quadrant : 32 * quadrant + 4].bitcast(I32),
                in_=Wf_scales[:, 4 * quadrant : 4 * quadrant + 4, :].bitcast(I32).rearrange("g r n -> r g n"),
            )
        load_pair(2)
        nc.sync.dma_start(out=w_words[:].bitcast(I32), in_=Wf_words.bitcast(I32).rearrange("g p b -> p g b"))
        load_pair(3)
        seen_sb = keep.tile([P, MEMORY_HALVES, FEATURES], BF16)
        nc.sync.dma_start(out=seen_sb[:], in_=seen.rearrange("(c m) j -> m c j", m=P))
        for pair in range(4, X_BUFS):
            load_pair(pair)

        bias_rows = keep.tile([P, P], BF16)
        nc.vector.memset(bias_rows[:], 0.0)
        nc.scalar.dma_start(out=bias_rows[0:PACK, :], in_=b_feat.rearrange("(t p) -> t p", p=P))

        one = keep.tile([P, 1], F32)
        nc.vector.memset(one[:], 1.0)
        nc.scalar.activation(out=one[:], in_=one[:], func=ACT.Sqrt)

        seen_grouped = keep.tile([P, MEMORY, PACK], BF16, align_bytes=64)
        seen_codes = keep.tile([P, MEMORY], U32, align_bytes=64)
        seen_scales = keep.tile([P, MEMORY], U8, align_bytes=64)
        half_s2 = keep.tile([P, MEMORY], F32)
        s2 = keep.tile([P, MEMORY_HALVES], F32)
        s2_repeated = keep.tile([P, MEMORY_HALVES, P], F32)
        bias = keep.tile([P, PACK], F32)

        def prepare_bias():
            bias_ps = psum4.tile([P, P], BF16, tag="feat")
            nc.tensor.transpose(bias_ps[:], bias_rows[:], ident_bf16[:])
            nc.vector.tensor_copy(out=bias[:], in_=bias_ps[:, 0:PACK])

        def transpose_memory():
            for c in range(MEMORY_HALVES):
                seen_ps = psum4.tile([P, PACK, P], BF16, tag="feat")
                for t in range(PACK):
                    nc.tensor.transpose(seen_ps[:, t, :], seen_sb[:, c, t * P : (t + 1) * P], ident_bf16[:])
                nc.vector.tensor_copy(
                    out=seen_grouped[:, c * P : (c + 1) * P, :], in_=seen_ps[:].rearrange("p t m -> p m t")
                )
                seen_squares = ring2.tile([P, FEATURES], F32)
                nc.scalar.activation(
                    out=seen_squares[:], in_=seen_sb[:, c, :], func=ACT.Square, accum_out=s2[:, c : c + 1]
                )
            for c in range(MEMORY_HALVES):
                nc.vector.tensor_copy(out=s2_repeated[:, c, :], in_=s2[:, c : c + 1].to_broadcast([P, P]))

        def quantise_memory():
            nc.vector.quantize_mx(
                out=seen_codes[:].bitcast(FP8X4),
                scales=seen_scales[:],
                in_=seen_grouped[:].rearrange("p m t -> p (m t)"),
            )

        def turn_memory_norms():
            s2_ps = psum4.tile([P, MEMORY_HALVES, P], F32, tag="feat")
            for c in range(MEMORY_HALVES):
                nc.tensor.transpose(s2_ps[:, c, :], s2_repeated[:, c, :], ident_f32[:])
            nc.vector.tensor_scalar_mul(out=half_s2[:], in0=s2_ps[:].rearrange("p c m -> p (c m)"), scalar1=0.5)

        a2 = keep.tile([P, GROUPS], F32)
        best = keep.tile([P, GROUPS], F32)

        def transpose_group(block, i):
            if i == 0:
                grouped = ring2.tile([P, K_PASSES, BLOCK_STATES, 2], F32, name="x_grouped", align_bytes=64)
                x_grouped[block] = grouped
            words = x_pairs[2 * block + i // 2][:, i % 2, :].bitcast(F32)
            xt = psum2.tile([P, K_PASSES, 2, P], F32)
            for g in range(K_PASSES):
                for u in range(2):
                    nc.tensor.transpose(xt[:, g, u, :], words[:, 256 * g + u : 256 * (g + 1) : 2], ident_f32[:])
            on_vector = i >= 2 if block == 1 else i > 0
            copy = nc.vector.tensor_copy if on_vector else nc.scalar.copy
            copy(
                out=x_grouped[block][:, :, i * P : (i + 1) * P, :], in_=xt[:].rearrange("p g u s -> p g s u")
            )

        def quantise_states(block):
            codes = ring2.tile([P, K_PASSES, BLOCK_STATES], U32, name="x_codes", align_bytes=64)
            scales = ring2.tile([P, K_PASSES, BLOCK_STATES], U8, name="x_scales", align_bytes=64)
            nc.vector.quantize_mx(
                out=codes[:].rearrange("p g s -> p (g s)").bitcast(FP8X4),
                scales=scales[:].rearrange("p g s -> p (g s)"),
                in_=x_grouped[block][:].rearrange("p g s u -> p (g s u)").bitcast(BF16),
            )
            x_codes[block], x_scales[block] = codes, scales

        def quantise_pair(block, half):
            if half == 0:
                codes = ring2.tile([P, K_PASSES, BLOCK_STATES], U32, name="x_codes", align_bytes=64)
                scales = ring2.tile([P, K_PASSES, BLOCK_STATES], U8, name="x_scales", align_bytes=64)
                x_codes[block], x_scales[block] = codes, scales
            states = slice(half * PAIR_STATES, (half + 1) * PAIR_STATES)
            for g in range(K_PASSES):
                nc.vector.quantize_mx(
                    out=x_codes[block][:, g, states].bitcast(FP8X4),
                    scales=x_scales[block][:, g, states],
                    in_=x_grouped[block][:, g, states, :].rearrange("p s u -> p (s u)").bitcast(BF16),
                )

        def features(block, t):
            if t == 0:
                fa = fa_pool.tile([P, PACK, BLOCK_STATES], F32)
                fa_blocks[block] = fa
            z = psum4.tile([P, BLOCK_STATES], F32, tag="feat")
            for g in range(K_PASSES):
                nc.tensor.matmul_mx(
                    out=z[:],
                    lhsT=w_words[:, g, 2 * P * t : 2 * P * (t + 1)].bitcast(FP4X4),
                    lhsT_scale=w_scales[:, g, P * t : P * (t + 1)],
                    rhs=x_codes[block][:, g, :].bitcast(FP8X4),
                    rhs_scale=x_scales[block][:, g, :],
                    start=(g == 0),
                    stop=(g == K_PASSES - 1),
                )
            nc.scalar.activation(out=fa_blocks[block][:, t, :], in_=z[:], func=ACT.Relu, bias=bias[:, t : t + 1])

        def regroup_features(pair, copy):
            cols = slice((pair % 2) * PAIR_STATES, (pair % 2 + 1) * PAIR_STATES)
            grouped = ring2.tile([P, PAIR_STATES, PACK], BF16, name="fa_grouped", align_bytes=64)
            copy(out=grouped[:], in_=fa_blocks[pair // 2][:, :, cols].rearrange("p t s -> p s t"))
            fa_grouped[pair] = grouped

        def gpsimd_copy(out, in_):
            nc.gpsimd.tensor_scalar(out=out, in0=in_, scalar1=1.0, scalar2=0.0, op0=ALU.mult, op1=ALU.add)

        def quantise_features(pair):
            codes = ring3.tile([P, PAIR_STATES], U32, name="fa_codes", align_bytes=64)
            scales = ring3.tile([P, PAIR_STATES], U8, name="fa_scales", align_bytes=64)
            nc.vector.quantize_mx(
                out=codes[:].bitcast(FP8X4), scales=scales[:], in_=fa_grouped[pair][:].rearrange("p s t -> p (s t)")
            )
            fa_codes[pair], fa_scales[pair] = codes, scales

        def square_norms(pair):
            for i in range(2):
                cols = slice((2 * (pair % 2) + i) * P, (2 * (pair % 2) + i + 1) * P)
                ft = psum4.tile([P, PACK, P], F32, tag="feat")
                for t in range(PACK):
                    nc.tensor.transpose(ft[:, t, :], fa_blocks[pair // 2][:, t, cols], ident_f32[:])
                squares = ring2.tile([P, FEATURES], F32)
                nc.scalar.activation(
                    out=squares[:],
                    in_=ft[:].rearrange("p t f -> p (t f)"),
                    func=ACT.Square,
                    accum_out=a2[:, 2 * pair + i : 2 * pair + i + 1],
                )

        def distances(pair):
            dot = psum2.tile([P, 2, MEMORY], F32)
            for i in range(2):
                nc.tensor.matmul_mx(
                    out=dot[:, i, :],
                    lhsT=fa_codes[pair][:, i * P : (i + 1) * P].bitcast(FP8X4),
                    lhsT_scale=fa_scales[pair][:, i * P : (i + 1) * P],
                    rhs=seen_codes[:].bitcast(FP8X4),
                    rhs_scale=seen_scales[:],
                    start=True,
                    stop=True,
                )
            dots[pair] = dot

        def subtract_norms(pair):
            margin = ring2.tile([P, 2, MEMORY], F32)
            nc.vector.tensor_tensor(
                out=margin[:],
                in0=dots[pair][:],
                in1=half_s2[:].unsqueeze(1).to_broadcast([P, 2, MEMORY]),
                op=ALU.subtract,
            )
            margins[pair] = margin

        def nearest(pair):
            nc.vector.tensor_reduce(
                out=best[:, 2 * pair : 2 * pair + 2], in_=margins[pair][:], axis=mybir.AxisListType.X, op=ALU.max
            )

        def is_pair(pair):
            return 0 <= pair < PAIRS

        def pipeline_step(step):
            new, now, old, done = step + 1, step, step - 1, step - 2
            for half in range(2):
                if step >= 0 and 2 * new + X_BUFS - 2 + half < PAIRS:
                    load_pair(2 * new + X_BUFS - 2 + half)
                if 0 <= old < BLOCKS:
                    regroup_features(2 * old + half, gpsimd_copy)
                if half == 0 and 0 <= done < BLOCKS:
                    subtract_norms(2 * done)
                for i in range(2):
                    if new < BLOCKS:
                        transpose_group(new, 2 * half + i)
                if half == 0 and 0 <= done < BLOCKS:
                    subtract_norms(2 * done + 1)
                    nearest(2 * done)
                    nearest(2 * done + 1)
                if is_pair(2 * step + half - NORM_LAG):
                    square_norms(2 * step + half - NORM_LAG)
                if step == -1 and half == 0:
                    prepare_bias()
                if step == 0 and half == 1:
                    transpose_memory()
                if step == 1 and half == 1:
                    turn_memory_norms()
                if half == 1:
                    if step == 1:
                        quantise_memory()
                    if 0 <= old < BLOCKS:
                        quantise_features(2 * old)
                        quantise_features(2 * old + 1)
                    if 0 < new < BLOCKS:
                        quantise_states(new)
                if new == 0:
                    quantise_pair(new, half)
                if 0 <= now < BLOCKS:
                    features(now, 2 * half)
                    features(now, 2 * half + 1)
            if 0 <= old < BLOCKS:
                distances(2 * old)
                distances(2 * old + 1)

        for step in range(-1, BLOCKS - 1):
            pipeline_step(step)

        last = BLOCKS - 1
        first, second, third, fourth = range(2 * last - 2, 2 * last + 2)
        regroup_features(first, gpsimd_copy)
        regroup_features(second, gpsimd_copy)
        for pair in (first - 2, first - 1):
            subtract_norms(pair)
        for pair in (first - 2, first - 1):
            nearest(pair)
        square_norms(third - NORM_LAG)
        features(last, 0)
        features(last, 1)
        features(last, 2)
        features(last, 3)
        quantise_features(first)
        quantise_features(second)
        distances(first)
        distances(second)
        regroup_features(third, nc.scalar.copy)
        regroup_features(fourth, gpsimd_copy)
        square_norms(fourth - NORM_LAG)
        subtract_norms(first)
        subtract_norms(second)
        nearest(first)
        quantise_features(third)
        quantise_features(fourth)
        square_norms(fourth - NORM_LAG + 1)
        distances(third)
        distances(fourth)
        nearest(second)
        subtract_norms(third)
        subtract_norms(fourth)
        nearest(third)
        nearest(fourth)
        for pair in range(fourth - NORM_LAG + 2, PAIRS):
            square_norms(pair)

        d2 = keep.tile([P, GROUPS], F32)
        nc.vector.scalar_tensor_tensor(out=d2[:], in0=best[:], scalar=-2.0, in1=a2[:], op0=ALU.mult, op1=ALU.add)
        nc.vector.tensor_scalar(out=d2[:], in0=d2[:], scalar1=SQRT_FLOOR, scalar2=100.0, op0=ALU.max, op1=ALU.min)
        novelty = keep.tile([P, GROUPS], F32)
        nc.scalar.activation(out=novelty[:], in_=d2[:], func=ACT.Sqrt, scale=0.01)
        nc.scalar.dma_start(out=out.rearrange("(p c) -> p c", c=GROUPS), in_=novelty[:])
